import numpy as np
import ml_dtypes


def mxq(x, axis, fmt="e4m3"):
    dtype, down = {"e4m3": (ml_dtypes.float8_e4m3fn, 7), "e5m2": (ml_dtypes.float8_e5m2, 14)}[fmt]
    v = np.moveaxis(np.asarray(x, np.float32).astype(ml_dtypes.bfloat16).astype(np.float64), axis, -1)
    blocks = v.reshape(v.shape[:-1] + (-1, 32))
    amax = np.abs(blocks).max(-1, keepdims=True)
    byte = np.maximum(np.where(amax > 0, np.frexp(amax)[1] - 1 + 127, 0) - down, 1)
    scale = np.exp2(byte - 127.0)
    codes = (blocks / scale).astype(np.float32).astype(dtype).astype(np.float64)
    return np.moveaxis((codes * scale).reshape(v.shape), -1, axis)


WIDE = False


def mx_kscale(k):
    if not WIDE:
        return np.ones(k)
    levels = np.array([10, -10, 5, -5, 0])
    a = np.random.permutation(np.resize(levels, k // 512 * 4)).reshape(k // 512, 4)
    idx = np.arange(k)
    return np.exp2(a[idx // 512, idx % 128 // 32])


BF16 = ml_dtypes.bfloat16


def bf(x):
    return np.asarray(x, np.float32).astype(BF16)


def f64(x):
    return np.asarray(x).astype(np.float64)


N, C, H, W, R = 2, 512, 32, 64, 512
HW = H * W


def sigmoid(z):
    return 1.0 / (1.0 + np.exp(-z))


def setup_inputs():
    sq, sk = mx_kscale(R), mx_kscale(R)
    return {"hq": bf(np.maximum(np.random.standard_normal((N, C, R)) * np.sqrt(2.0), 0.0) * sq),
            "hk": bf(np.maximum(np.random.standard_normal((N, C, R)) * np.sqrt(2.0), 0.0) * sk),
            "wq2": bf(np.random.standard_normal((R, HW)) * 3.0 / np.sqrt(R) / sq[:, None]),
            "wk2": bf(np.random.standard_normal((R, HW)) * 3.0 / np.sqrt(R) / sk[:, None])}


def reference(hq, hk, wq2, wk2):
    q = sigmoid(mxq(f64(hq), 2, "e4m3") @ mxq(f64(wq2), 0, "e4m3"))
    k = sigmoid(mxq(f64(hk), 2, "e4m3") @ mxq(f64(wk2), 0, "e4m3"))
    s = (mxq(q, 2, "e4m3") @ mxq(k, 2, "e4m3").transpose(0, 2, 1)) / np.sqrt(C)
    ex = np.exp(s - s.max(-1, keepdims=True))
    return ex / ex.sum(-1, keepdims=True)

@@ -1,0 +1,251 @@
+from contextlib import ExitStack
+import math
+
+import concourse.mybir as mybir
+from concourse.masks import make_identity
+
+F32 = mybir.dt.float32
+BF16 = mybir.dt.bfloat16
+U32 = mybir.dt.uint32
+U8 = mybir.dt.uint8
+FP8X4 = mybir.dt.float8_e4m3fn_x4
+AF = mybir.ActivationFunctionType
+ALU = mybir.AluOpType
+AX = mybir.AxisListType
+
+P = 128
+IMAGES = 2
+C = 512
+R = 512
+HW = 2048
+K_PASS = 512
+G = HW // K_PASS
+CB = C // P
+UNITS = 4 * G
+FLOPS = 2 * 2 * IMAGES * C * R * HW + 2 * IMAGES * C * C * HW
+
+
+def tile_complexchannelattn_pa_kernel(tc, hq, hk, wq2, wk2, out):
+    nc = tc.nc
+    h_dram = (hq, hk)
+    w_dram = (wq2, wk2)
+    inv = 1.0 / math.sqrt(C)
+    with ExitStack() as ctx:
+        keep = ctx.enter_context(tc.tile_pool(name="keep", bufs=1))
+        wgp = ctx.enter_context(tc.tile_pool(name="wgp", bufs=2))
+        hgp = ctx.enter_context(tc.tile_pool(name="hgp", bufs=2))
+        agp = ctx.enter_context(tc.tile_pool(name="agp", bufs=8))
+        rot = ctx.enter_context(tc.psum_pool(name="rot", bufs=4))
+        acc = ctx.enter_context(tc.psum_pool(name="acc", bufs=4))
+        ctx.enter_context(tc.manual_schedule())
+
+        h_raw = [[[keep.tile([P, 2 * R], BF16, name="hraw%d%d%d" % (x, n, f)) for f in range(2)]
+                  for n in range(IMAGES)] for x in range(2)]
+        w_raw = [[keep.tile([P, 4, K_PASS], BF16, name="wraw%d%d" % (x, g)) for g in range(G)]
+                 for x in range(2)]
+        h_codes = [[keep.tile([P, C], U32, name="hc%d%d" % (x, n), align_bytes=64)
+                    for n in range(IMAGES)] for x in range(2)]
+        h_scales = [[keep.tile([P, C], U8, name="hs%d%d" % (x, n), align_bytes=64)
+                     for n in range(IMAGES)] for x in range(2)]
+        w_codes = [keep.tile([P, HW], U32, name="wc%d" % x, align_bytes=64) for x in range(2)]
+        w_scales = [keep.tile([P, HW], U8, name="ws%d" % x, align_bytes=64) for x in range(2)]
+        a_codes = [[keep.tile([P, G, C], U32, name="ac%d%d" % (x, n), align_bytes=64)
+                    for n in range(IMAGES)] for x in range(2)]
+        a_scales = [[keep.tile([P, G, C], U8, name="as%d%d" % (x, n), align_bytes=64)
+                     for n in range(IMAGES)] for x in range(2)]
+        s_sb = [keep.tile([P, C], F32, name="ssb%d" % m) for m in range(CB)]
+        e_sb = [[keep.tile([P, C], F32, name="e%d%d" % (n, m)) for m in range(CB)]
+                for n in range(IMAGES)]
+        mx = [[keep.tile([P, 1], F32, name="mx%d%d" % (n, m)) for m in range(CB)] for n in range(IMAGES)]
+        nb = [[keep.tile([P, 1], F32, name="nb%d%d" % (n, m)) for m in range(CB)] for n in range(IMAGES)]
+        sm = [[keep.tile([P, 1], F32, name="sm%d%d" % (n, m)) for m in range(CB)] for n in range(IMAGES)]
+        rs = [[keep.tile([P, 1], F32, name="rs%d%d" % (n, m)) for m in range(CB)] for n in range(IMAGES)]
+        ident = keep.tile([P, P], F32, name="ident")
+        warm_in = keep.tile([P, 1], F32, name="warm_in")
+        warm_out = keep.tile([P, 1], F32, name="warm_out")
+
+        def load_h(x, n, f):
+            nc.sync.dma_start(
+                out=h_raw[x][n][f][:].rearrange("p (b r) -> p b r", b=2),
+                in_=h_dram[x][n, 2 * P * f:2 * P * (f + 1), :].rearrange("(b p) r -> p b r", p=P),
+            )
+
+        def load_w(x, g):
+            for u in range(2):
+                nc.sync.dma_start(
+                    out=w_raw[x][g][:, 2 * u:2 * u + 2, :],
+                    in_=w_dram[x][2 * P * u:2 * P * (u + 1), K_PASS * g:K_PASS * (g + 1)].rearrange(
+                        "(p e) c -> p e c", e=2),
+                )
+
+        load_h(0, 0, 0)
+        load_w(0, 0)
+        load_h(0, 0, 1)
+        for g in range(1, G):
+            load_w(0, g)
+        load_h(1, 0, 0)
+        load_h(1, 0, 1)
+        for g in range(G):
+            load_w(1, g)
+        for x in range(2):
+            for f in range(2):
+                load_h(x, 1, f)
+
+        make_identity(nc, ident[:])
+        nc.vector.memset(warm_in[:], 0.0)
+        nc.scalar.activation(out=warm_out[:], in_=warm_in[:], func=AF.Sigmoid)
+
+        def h_transposes(x, n, f):
+            xt = acc.tile([P, 2, 2, P], F32, tag="acc", name="xt")
+            words = h_raw[x][n][f][:].bitcast(F32)
+            for b in range(2):
+                for u in range(2):
+                    lo = 2 * P * b + P * u
+                    nc.tensor.transpose(xt[:, b, u, :], words[:, lo:lo + P], ident[:])
+            return xt
+
+        def h_copy(copy, xt, hg, f):
+            dst = hg[:].bitcast(F32)[:, 4 * P * f:4 * P * (f + 1)]
+            copy(out=dst.rearrange("p (b c u) -> p b c u", b=2, u=2),
+                 in_=xt[:].rearrange("p b u c -> p b c u"))
+
+        def h_quant(x, n, hg, f):
+            cols = slice(2 * P * f, 2 * P * (f + 1))
+            nc.vector.quantize_mx(out=h_codes[x][n][:, cols].bitcast(FP8X4),
+                                  scales=h_scales[x][n][:, cols],
+                                  in_=hg[:, 8 * P * f:8 * P * (f + 1)])
+
+        def w_regroup(copy, x, g, wg, m0, m1):
+            copy(out=wg[:, m0:m1, :].rearrange("p (c i) t -> p c t i", i=4),
+                 in_=w_raw[x][g][:, :, m0:m1].rearrange("p t (c i) -> p c t i", i=4))
+
+        def w_quant(x, g, wg, m0, m1):
+            cols = slice(K_PASS * g + m0, K_PASS * g + m1)
+            nc.vector.quantize_mx(out=w_codes[x][:, cols].bitcast(FP8X4),
+                                  scales=w_scales[x][:, cols],
+                                  in_=wg[:, m0:m1, :].rearrange("p m t -> p (m t)"))
+
+        def prep_h(x, n):
+            xts = [h_transposes(x, n, f) for f in range(2)]
+            hg = hgp.tile([P, 4 * C], BF16, name="hg", align_bytes=64)
+            for f in range(2):
+                h_copy(nc.vector.tensor_copy, xts[f], hg, f)
+            for f in range(2):
+                h_quant(x, n, hg, f)
+
+        def prep_w(x, g):
+            wg = wgp.tile([P, K_PASS, 4], BF16, name="wg", align_bytes=64)
+            half = K_PASS // 2
+            for f in range(2):
+                w_regroup(nc.vector.tensor_copy, x, g, wg, half * f, half * (f + 1))
+            for f in range(2):
+                w_quant(x, g, wg, half * f, half * (f + 1))
+
+        def a_quant(x, n, g, ag, c0, c1):
+            nc.vector.quantize_mx(out=a_codes[x][n][:, g, c0:c1].bitcast(FP8X4),
+                                  scales=a_scales[x][n][:, g, c0:c1],
+                                  in_=ag[:, 4 * c0:4 * c1])
+
+        def unit_of(u):
+            return u // (2 * G), (u // G) % 2, u % G
+
+        ags = {}
+
+        def run_unit(u, quantise_each_bank):
+            n, x, g = unit_of(u)
+            ag = agp.tile([P, 4 * C], BF16, name="ag", align_bytes=64)
+            ags[u] = ag
+            for cb in range(CB):
+                bank = rot.tile([P, 4, P], F32, tag="rot", name="bank")
+                for j in range(4):
+                    wcols = slice(K_PASS * g + P * j, K_PASS * g + P * (j + 1))
+                    hcols = slice(P * cb, P * (cb + 1))
+                    nc.tensor.matmul_mx(out=bank[:, j, :],
+                                        lhsT=w_codes[x][:, wcols].bitcast(FP8X4),
+                                        lhsT_scale=w_scales[x][:, wcols],
+                                        rhs=h_codes[x][n][:, hcols].bitcast(FP8X4),
+                                        rhs_scale=h_scales[x][n][:, hcols],
+                                        start=True, stop=True)
+                nc.scalar.activation(
+                    out=ag[:, 4 * P * cb:4 * P * (cb + 1)].rearrange("p (c j) -> p c j", j=4),
+                    in_=bank[:].rearrange("p j c -> p c j"), func=AF.Sigmoid)
+                if quantise_each_bank:
+                    a_quant(x, n, g, ag, P * cb, P * (cb + 1))
+
+        def quantise_unit(u):
+            n, x, g = unit_of(u)
+            a_quant(x, n, g, ags[u], 0, C)
+
+        s_ps = {}
+
+        def scores(n, g):
+            for m in range(CB):
+                if g == 0:
+                    s_ps[(n, m)] = acc.tile([P, C], F32, tag="acc", name="s")
+                mcols = slice(P * m, P * (m + 1))
+                nc.tensor.matmul_mx(out=s_ps[(n, m)][:],
+                                    lhsT=a_codes[0][n][:, g, mcols].bitcast(FP8X4),
+                                    lhsT_scale=a_scales[0][n][:, g, mcols],
+                                    rhs=a_codes[1][n][:, g, :].bitcast(FP8X4),
+                                    rhs_scale=a_scales[1][n][:, g, :],
+                                    start=(g == 0), stop=(g == G - 1))
+
+        def finish(n, m):
+            nc.vector.reciprocal(out=rs[n][m][:], in_=sm[n][m][:])
+            nc.vector.tensor_scalar(out=e_sb[n][m][:], in0=e_sb[n][m][:], scalar1=rs[n][m][:],
+                                    scalar2=None, op0=ALU.mult)
+            nc.sync.dma_start(out=out[n, P * m:P * (m + 1), :], in_=e_sb[n][m][:])
+
+        xt_a = h_transposes(0, 0, 0)
+        xt_b = h_transposes(0, 0, 1)
+        hg0 = hgp.tile([P, 4 * C], BF16, name="hg", align_bytes=64)
+        wg0 = wgp.tile([P, K_PASS, 4], BF16, name="wg", align_bytes=64)
+        h_copy(nc.scalar.copy, xt_a, hg0, 0)
+        w_regroup(nc.vector.tensor_copy, 0, 0, wg0, 0, 3 * P)
+        w_regroup(nc.scalar.copy, 0, 0, wg0, 3 * P, 4 * P)
+        h_quant(0, 0, hg0, 0)
+        w_quant(0, 0, wg0, 0, K_PASS)
+        h_copy(nc.scalar.copy, xt_b, hg0, 1)
+        h_quant(0, 0, hg0, 1)
+
+        preps = {0: [("w", 0, 1)], 1: [("w", 0, 2)], 2: [("w", 0, 3)], 3: [("h", 1, 0), ("w", 1, 0)],
+                 4: [("w", 1, 1)], 5: [("w", 1, 2)], 6: [("w", 1, 3), ("h", 0, 1)], 7: [("h", 1, 1)]}
+        quants = {6: [0, 4, 1, 5], 7: [2, 6, 3, 7]}
+        score_at = {8: [(0, 0)], 9: [(0, 1)], 10: [(0, 2)], 11: [(0, 3)], 14: [(1, 0)],
+                    15: [(1, 1), (1, 2)]}
+
+        for u in range(UNITS):
+            for kind, x, i in preps.get(u, []):
+                if kind == "w":
+                    prep_w(x, i)
+                else:
+                    prep_h(x, i)
+            run_unit(u, u == UNITS - 1)
+            for n, g in score_at.get(u, []):
+                scores(n, g)
+            if u == 11:
+                for m in range(CB):
+                    nc.vector.tensor_scalar(out=s_sb[m][:], in0=s_ps[(0, m)][:], scalar1=inv,
+                                            scalar2=None, op0=ALU.mult, op1=ALU.max,
+                                            accum_out=mx[0][m][:])
+                    nc.vector.tensor_scalar(out=nb[0][m][:], in0=mx[0][m][:], scalar1=-1.0,
+                                            scalar2=None, op0=ALU.mult)
+            if u >= 8 and u < UNITS - 1:
+                quantise_unit(u)
+            for v in quants.get(u, []):
+                quantise_unit(v)
+
+        scores(1, G - 1)
+        for m in range(CB):
+            nc.vector.tensor_reduce(out=mx[1][m][:], in_=s_ps[(1, m)][:], axis=AX.X, op=ALU.max)
+            nc.vector.tensor_scalar(out=nb[1][m][:], in0=mx[1][m][:], scalar1=-inv,
+                                    scalar2=None, op0=ALU.mult)
+        for m in range(CB):
+            nc.scalar.activation(out=e_sb[0][m][:], in_=s_sb[m][:], func=AF.Exp,
+                                 bias=nb[0][m][:], scale=1.0, accum_out=sm[0][m][:])
+        for m in range(CB):
+            nc.scalar.activation(out=e_sb[1][m][:], in_=s_ps[(1, m)][:], func=AF.Exp,
+                                 bias=nb[1][m][:], scale=inv, accum_out=sm[1][m][:])
+        for n in range(IMAGES):
+            for m in range(CB):
+                finish(n, m)

@@ -22,6 +22,18 @@ K_PASS = 512
 G = HW // K_PASS
 CB = C // P
 UNITS = 4 * G
+DRAIN = -1
+HEAD_SPLIT = 64
+ORDER = [(0, 0, 0), (0, 0, 1), (0, 0, 2), (0, 0, 3), (1, 0, 0), (1, 0, 1), (0, 1, 0), (0, 1, 1),
+         (0, 1, 2), (0, 1, 3), (1, 0, 2), (1, 0, 3), (1, 1, 0), (1, 1, 1), (1, 1, 2), (1, 1, 3)]
+LOADS = [("h", 0, 0, 0), ("w", 0, 0, 0), ("w", 0, 0, 256), ("h", 0, 0, 1), ("h", 0, 0, 2), ("h", 0, 0, 3),
+         ("w", 0, 1, 0), ("w", 0, 1, 256), ("w", 0, 2, 0), ("w", 0, 3, 0), ("h", 0, 1, 0), ("h", 0, 1, 2),
+         ("h", 1, 0, 0), ("h", 1, 0, 2), ("w", 1, 0, 0), ("w", 1, 1, 0), ("h", 1, 1, 0), ("h", 1, 1, 2),
+         ("w", 1, 2, 0), ("w", 1, 3, 0)]
+BEFORE = {1: [("w", 0, 2)], 2: [("w", 0, 3)], 3: [("h", 0, 1)], 4: [("h", 1, 0)],
+          5: [("w", 1, 0)], 6: [("w", 1, 1), ("h", 1, 1)], 7: [("w", 1, 2)], 8: [("w", 1, 3)]}
+AFTER = {8: [0, 6], 9: [1, 7, 2, 8, 3, 9], 10: [4, 5, 10], 11: [11], 12: [DRAIN, 12], 13: [13], 14: [14]}
+SCORES = {9: [(0, 0)], 10: [(0, 1)], 11: [(0, 2)], 12: [(0, 3)], 14: [(1, 0)], 15: [(1, 1), (1, 2)]}
 FLOPS = 2 * 2 * IMAGES * C * R * HW + 2 * IMAGES * C * C * HW
 
 
@@ -39,10 +51,12 @@ def tile_complexchannelattn_pa_kernel(tc, hq, hk, wq2, wk2, out):
         acc = ctx.enter_context(tc.psum_pool(name="acc", bufs=4))
         ctx.enter_context(tc.manual_schedule())
 
-        h_raw = [[[keep.tile([P, 2 * R], BF16, name="hraw%d%d%d" % (x, n, f)) for f in range(2)]
-                  for n in range(IMAGES)] for x in range(2)]
-        w_raw = [[keep.tile([P, 4, K_PASS], BF16, name="wraw%d%d" % (x, g)) for g in range(G)]
-                 for x in range(2)]
+        h_step = {(x, n): (1 if (x, n) == (0, 0) else 2) for x in range(2) for n in range(IMAGES)}
+        h_raw = {(x, n, b): keep.tile([P, h_step[(x, n)] * R], BF16, name="hraw%d%d%d" % (x, n, b))
+                 for x in range(2) for n in range(IMAGES) for b in range(0, CB, h_step[(x, n)])}
+        w_step = {(x, g): (K_PASS // 2 if (x, g) in ((0, 0), (0, 1)) else K_PASS) for x in range(2) for g in range(G)}
+        w_raw = {(x, g, m): keep.tile([P, 4, w_step[(x, g)]], BF16, name="wraw%d%d%d" % (x, g, m))
+                 for x in range(2) for g in range(G) for m in range(0, K_PASS, w_step[(x, g)])}
         h_codes = [[keep.tile([P, C], U32, name="hc%d%d" % (x, n), align_bytes=64)
                     for n in range(IMAGES)] for x in range(2)]
         h_scales = [[keep.tile([P, C], U8, name="hs%d%d" % (x, n), align_bytes=64)
@@ -64,60 +78,59 @@ def tile_complexchannelattn_pa_kernel(tc, hq, hk, wq2, wk2, out):
         warm_in = keep.tile([P, 1], F32, name="warm_in")
         warm_out = keep.tile([P, 1], F32, name="warm_out")
 
-        def load_h(x, n, f):
+        def load_h(x, n, b):
+            span = h_step[(x, n)]
             nc.sync.dma_start(
-                out=h_raw[x][n][f][:].rearrange("p (b r) -> p b r", b=2),
-                in_=h_dram[x][n, 2 * P * f:2 * P * (f + 1), :].rearrange("(b p) r -> p b r", p=P),
+                out=h_raw[(x, n, b)][:].rearrange("p (b r) -> p b r", b=span),
+                in_=h_dram[x][n, P * b:P * (b + span), :].rearrange("(b p) r -> p b r", p=P),
             )
 
-        def load_w(x, g):
+        def load_w(x, g, m):
+            lo = K_PASS * g + m
             for u in range(2):
                 nc.sync.dma_start(
-                    out=w_raw[x][g][:, 2 * u:2 * u + 2, :],
-                    in_=w_dram[x][2 * P * u:2 * P * (u + 1), K_PASS * g:K_PASS * (g + 1)].rearrange(
+                    out=w_raw[(x, g, m)][:, 2 * u:2 * u + 2, :],
+                    in_=w_dram[x][2 * P * u:2 * P * (u + 1), lo:lo + w_step[(x, g)]].rearrange(
                         "(p e) c -> p e c", e=2),
                 )
 
-        load_h(0, 0, 0)
-        load_w(0, 0)
-        load_h(0, 0, 1)
-        for g in range(1, G):
-            load_w(0, g)
-        load_h(1, 0, 0)
-        load_h(1, 0, 1)
-        for g in range(G):
-            load_w(1, g)
-        for x in range(2):
-            for f in range(2):
-                load_h(x, 1, f)
+        for what in LOADS:
+            if what[0] == "h":
+                load_h(what[1], what[2], what[3])
+            else:
+                load_w(what[1], what[2], what[3])
 
         make_identity(nc, ident[:])
         nc.vector.memset(warm_in[:], 0.0)
         nc.scalar.activation(out=warm_out[:], in_=warm_in[:], func=AF.Sigmoid)
 
-        def h_transposes(x, n, f):
-            xt = acc.tile([P, 2, 2, P], F32, tag="acc", name="xt")
-            words = h_raw[x][n][f][:].bitcast(F32)
-            for b in range(2):
+        def h_transposes(x, n, b0):
+            span = h_step[(x, n)]
+            xt = acc.tile([P, span, 2, P], F32, tag="acc", name="xt")
+            words = h_raw[(x, n, b0)][:].bitcast(F32)
+            for b in range(span):
                 for u in range(2):
                     lo = 2 * P * b + P * u
                     nc.tensor.transpose(xt[:, b, u, :], words[:, lo:lo + P], ident[:])
             return xt
 
-        def h_copy(copy, xt, hg, f):
-            dst = hg[:].bitcast(F32)[:, 4 * P * f:4 * P * (f + 1)]
-            copy(out=dst.rearrange("p (b c u) -> p b c u", b=2, u=2),
+        def h_copy(copy, x, n, xt, hg, b0):
+            span = h_step[(x, n)]
+            dst = hg[:].bitcast(F32)[:, 2 * P * b0:2 * P * (b0 + span)]
+            copy(out=dst.rearrange("p (b c u) -> p b c u", b=span, u=2),
                  in_=xt[:].rearrange("p b u c -> p b c u"))
 
-        def h_quant(x, n, hg, f):
-            cols = slice(2 * P * f, 2 * P * (f + 1))
+        def h_quant(x, n, hg, b0):
+            span = h_step[(x, n)]
+            cols = slice(P * b0, P * (b0 + span))
             nc.vector.quantize_mx(out=h_codes[x][n][:, cols].bitcast(FP8X4),
                                   scales=h_scales[x][n][:, cols],
-                                  in_=hg[:, 8 * P * f:8 * P * (f + 1)])
+                                  in_=hg[:, 4 * P * b0:4 * P * (b0 + span)])
 
         def w_regroup(copy, x, g, wg, m0, m1):
+            base = m0 - m0 % w_step[(x, g)]
             copy(out=wg[:, m0:m1, :].rearrange("p (c i) t -> p c t i", i=4),
-                 in_=w_raw[x][g][:, :, m0:m1].rearrange("p t (c i) -> p c t i", i=4))
+                 in_=w_raw[(x, g, base)][:, :, m0 - base:m1 - base].rearrange("p t (c i) -> p c t i", i=4))
 
         def w_quant(x, g, wg, m0, m1):
             cols = slice(K_PASS * g + m0, K_PASS * g + m1)
@@ -126,12 +139,12 @@ def tile_complexchannelattn_pa_kernel(tc, hq, hk, wq2, wk2, out):
                                   in_=wg[:, m0:m1, :].rearrange("p m t -> p (m t)"))
 
         def prep_h(x, n):
-            xts = [h_transposes(x, n, f) for f in range(2)]
+            xts = [h_transposes(x, n, b) for b in range(0, CB, 2)]
             hg = hgp.tile([P, 4 * C], BF16, name="hg", align_bytes=64)
-            for f in range(2):
-                h_copy(nc.vector.tensor_copy, xts[f], hg, f)
-            for f in range(2):
-                h_quant(x, n, hg, f)
+            for b in range(0, CB, 2):
+                h_copy(nc.vector.tensor_copy, x, n, xts[b // 2], hg, b)
+            for b in range(0, CB, 2):
+                h_quant(x, n, hg, b)
 
         def prep_w(x, g):
             wg = wgp.tile([P, K_PASS, 4], BF16, name="wg", align_bytes=64)
@@ -147,15 +160,17 @@ def tile_complexchannelattn_pa_kernel(tc, hq, hk, wq2, wk2, out):
                                   in_=ag[:, 4 * c0:4 * c1])
 
         def unit_of(u):
-            return u // (2 * G), (u // G) % 2, u % G
+            return ORDER[u]
 
         ags = {}
 
-        def run_unit(u, quantise_each_bank):
+        def run_unit(u, quantise_each_bank, before_bank):
             n, x, g = unit_of(u)
             ag = agp.tile([P, 4 * C], BF16, name="ag", align_bytes=64)
             ags[u] = ag
             for cb in range(CB):
+                if cb in before_bank:
+                    before_bank[cb]()
                 bank = rot.tile([P, 4, P], F32, tag="rot", name="bank")
                 for j in range(4):
                     wcols = slice(K_PASS * g + P * j, K_PASS * g + P * (j + 1))
@@ -196,56 +211,66 @@ def tile_complexchannelattn_pa_kernel(tc, hq, hk, wq2, wk2, out):
                                     scalar2=None, op0=ALU.mult)
             nc.sync.dma_start(out=out[n, P * m:P * (m + 1), :], in_=e_sb[n][m][:])
 
-        xt_a = h_transposes(0, 0, 0)
-        xt_b = h_transposes(0, 0, 1)
         hg0 = hgp.tile([P, 4 * C], BF16, name="hg", align_bytes=64)
         wg0 = wgp.tile([P, K_PASS, 4], BF16, name="wg", align_bytes=64)
-        h_copy(nc.scalar.copy, xt_a, hg0, 0)
-        w_regroup(nc.vector.tensor_copy, 0, 0, wg0, 0, 3 * P)
-        w_regroup(nc.scalar.copy, 0, 0, wg0, 3 * P, 4 * P)
-        h_quant(0, 0, hg0, 0)
-        w_quant(0, 0, wg0, 0, K_PASS)
-        h_copy(nc.scalar.copy, xt_b, hg0, 1)
-        h_quant(0, 0, hg0, 1)
+        half = K_PASS // 2
+        def head_block(b, copy):
+            xt = h_transposes(0, 0, b)
+            h_copy(copy, 0, 0, xt, hg0, b)
+            h_quant(0, 0, hg0, b)
 
-        preps = {0: [("w", 0, 1)], 1: [("w", 0, 2)], 2: [("w", 0, 3)], 3: [("h", 1, 0), ("w", 1, 0)],
-                 4: [("w", 1, 1)], 5: [("w", 1, 2)], 6: [("w", 1, 3), ("h", 0, 1)], 7: [("h", 1, 1)]}
-        quants = {6: [0, 4, 1, 5], 7: [2, 6, 3, 7]}
-        score_at = {8: [(0, 0)], 9: [(0, 1)], 10: [(0, 2)], 11: [(0, 3)], 14: [(1, 0)],
-                    15: [(1, 1), (1, 2)]}
+        head_block(0, nc.scalar.copy)
+        w_regroup(nc.vector.tensor_copy, 0, 0, wg0, 0, half)
+        w_quant(0, 0, wg0, 0, half)
+        w_regroup(nc.vector.tensor_copy, 0, 0, wg0, half, half + P // 2 + HEAD_SPLIT)
+        w_regroup(nc.scalar.copy, 0, 0, wg0, half + P // 2 + HEAD_SPLIT, K_PASS)
+        w_quant(0, 0, wg0, half, K_PASS)
+        head_block(1, nc.scalar.copy)
+        head_block(2, nc.scalar.copy)
+        head_block(3, nc.vector.tensor_copy)
+        late_blocks = {}
 
         for u in range(UNITS):
-            for kind, x, i in preps.get(u, []):
+            for kind, x, i in BEFORE.get(u, []):
                 if kind == "w":
                     prep_w(x, i)
                 else:
                     prep_h(x, i)
-            run_unit(u, u == UNITS - 1)
-            for n, g in score_at.get(u, []):
+            run_unit(u, u == UNITS - 1, late_blocks if u == 0 else {})
+            if u == 0:
+                prep_w(0, 1)
+            for n, g in SCORES.get(u, []):
                 scores(n, g)
-            if u == 11:
-                for m in range(CB):
-                    nc.vector.tensor_scalar(out=s_sb[m][:], in0=s_ps[(0, m)][:], scalar1=inv,
-                                            scalar2=None, op0=ALU.mult, op1=ALU.max,
-                                            accum_out=mx[0][m][:])
-                    nc.vector.tensor_scalar(out=nb[0][m][:], in0=mx[0][m][:], scalar1=-1.0,
-                                            scalar2=None, op0=ALU.mult)
-            if u >= 8 and u < UNITS - 1:
-                quantise_unit(u)
-            for v in quants.get(u, []):
-                quantise_unit(v)
+            for v in AFTER.get(u, []):
+                if v == DRAIN:
+                    for m in range(CB):
+                        nc.vector.tensor_scalar(out=s_sb[m][:], in0=s_ps[(0, m)][:], scalar1=inv,
+                                                scalar2=None, op0=ALU.mult, op1=ALU.max,
+                                                accum_out=mx[0][m][:])
+                        nc.vector.tensor_scalar(out=nb[0][m][:], in0=mx[0][m][:], scalar1=-1.0,
+                                                scalar2=None, op0=ALU.mult)
+                else:
+                    quantise_unit(v)
 
-        scores(1, G - 1)
-        for m in range(CB):
+        def row_max(m):
             nc.vector.tensor_reduce(out=mx[1][m][:], in_=s_ps[(1, m)][:], axis=AX.X, op=ALU.max)
             nc.vector.tensor_scalar(out=nb[1][m][:], in0=mx[1][m][:], scalar1=-inv,
                                     scalar2=None, op0=ALU.mult)
+
+        scores(1, G - 1)
+        row_max(0)
+        row_max(1)
         for m in range(CB):
             nc.scalar.activation(out=e_sb[0][m][:], in_=s_sb[m][:], func=AF.Exp,
                                  bias=nb[0][m][:], scale=1.0, accum_out=sm[0][m][:])
         for m in range(CB):
+            nc.vector.reciprocal(out=rs[0][m][:], in_=sm[0][m][:])
+            if m + 2 < CB:
+                row_max(m + 2)
+            nc.gpsimd.tensor_scalar(out=e_sb[0][m][:], in0=e_sb[0][m][:], scalar1=rs[0][m][:],
+                                    scalar2=0.0, op0=ALU.mult, op1=ALU.add)
+            nc.sync.dma_start(out=out[0, P * m:P * (m + 1), :], in_=e_sb[0][m][:])
+        for m in range(CB):
             nc.scalar.activation(out=e_sb[1][m][:], in_=s_ps[(1, m)][:], func=AF.Exp,
                                  bias=nb[1][m][:], scale=inv, accum_out=sm[1][m][:])
-        for n in range(IMAGES):
-            for m in range(CB):
-                finish(n, m)
+            finish(1, m)

@@ -23,13 +23,9 @@ G = HW // K_PASS
 CB = C // P
 UNITS = 4 * G
 DRAIN = -1
-HEAD_SPLIT = 64
+HEAD_SPLIT = 352
 ORDER = [(0, 0, 0), (0, 0, 1), (0, 0, 2), (0, 0, 3), (1, 0, 0), (1, 0, 1), (0, 1, 0), (0, 1, 1),
          (0, 1, 2), (0, 1, 3), (1, 0, 2), (1, 0, 3), (1, 1, 0), (1, 1, 1), (1, 1, 2), (1, 1, 3)]
-LOADS = [("h", 0, 0, 0), ("w", 0, 0, 0), ("w", 0, 0, 256), ("h", 0, 0, 1), ("h", 0, 0, 2), ("h", 0, 0, 3),
-         ("w", 0, 1, 0), ("w", 0, 1, 256), ("w", 0, 2, 0), ("w", 0, 3, 0), ("h", 0, 1, 0), ("h", 0, 1, 2),
-         ("h", 1, 0, 0), ("h", 1, 0, 2), ("w", 1, 0, 0), ("w", 1, 1, 0), ("h", 1, 1, 0), ("h", 1, 1, 2),
-         ("w", 1, 2, 0), ("w", 1, 3, 0)]
 BEFORE = {1: [("w", 0, 2)], 2: [("w", 0, 3)], 3: [("h", 0, 1)], 4: [("h", 1, 0)],
           5: [("w", 1, 0)], 6: [("w", 1, 1), ("h", 1, 1)], 7: [("w", 1, 2)], 8: [("w", 1, 3)]}
 AFTER = {8: [0, 6], 9: [1, 7, 2, 8, 3, 9], 10: [4, 5, 10], 11: [11], 12: [DRAIN, 12], 13: [13], 14: [14]}
@@ -51,12 +47,10 @@ def tile_complexchannelattn_pa_kernel(tc, hq, hk, wq2, wk2, out):
         acc = ctx.enter_context(tc.psum_pool(name="acc", bufs=4))
         ctx.enter_context(tc.manual_schedule())
 
-        h_step = {(x, n): (1 if (x, n) == (0, 0) else 2) for x in range(2) for n in range(IMAGES)}
-        h_raw = {(x, n, b): keep.tile([P, h_step[(x, n)] * R], BF16, name="hraw%d%d%d" % (x, n, b))
-                 for x in range(2) for n in range(IMAGES) for b in range(0, CB, h_step[(x, n)])}
-        w_step = {(x, g): (K_PASS // 2 if (x, g) in ((0, 0), (0, 1)) else K_PASS) for x in range(2) for g in range(G)}
-        w_raw = {(x, g, m): keep.tile([P, 4, w_step[(x, g)]], BF16, name="wraw%d%d%d" % (x, g, m))
-                 for x in range(2) for g in range(G) for m in range(0, K_PASS, w_step[(x, g)])}
+        h_raw = {(x, n): keep.tile([P, CB * R], BF16, name="hraw%d%d" % (x, n))
+                 for x in range(2) for n in range(IMAGES)}
+        wq_raw = [keep.tile([P, 4, K_PASS], BF16, name="wqraw%d" % g) for g in range(G)]
+        wk_raw = keep.tile([P, 4, HW], BF16, name="wkraw")
         h_codes = [[keep.tile([P, C], U32, name="hc%d%d" % (x, n), align_bytes=64)
                     for n in range(IMAGES)] for x in range(2)]
         h_scales = [[keep.tile([P, C], U8, name="hs%d%d" % (x, n), align_bytes=64)
@@ -78,59 +72,64 @@ def tile_complexchannelattn_pa_kernel(tc, hq, hk, wq2, wk2, out):
         warm_in = keep.tile([P, 1], F32, name="warm_in")
         warm_out = keep.tile([P, 1], F32, name="warm_out")
 
-        def load_h(x, n, b):
-            span = h_step[(x, n)]
-            nc.sync.dma_start(
-                out=h_raw[(x, n, b)][:].rearrange("p (b r) -> p b r", b=span),
-                in_=h_dram[x][n, P * b:P * (b + span), :].rearrange("(b p) r -> p b r", p=P),
-            )
+        def load_h(x, n):
+            if x == 0:
+                src = h_dram[x][n].rearrange("(p b) r -> p (b r)", b=CB)
+                nc.sync.dma_start(out=h_raw[(x, n)][:], in_=src)
+            else:
+                src = h_dram[x][n].rearrange("(b p) r -> p b r", p=P)
+                nc.sync.dma_start(out=h_raw[(x, n)][:].rearrange("p (b r) -> p b r", b=CB), in_=src)
 
-        def load_w(x, g, m):
-            lo = K_PASS * g + m
+        def load_wq(g):
             for u in range(2):
                 nc.sync.dma_start(
-                    out=w_raw[(x, g, m)][:, 2 * u:2 * u + 2, :],
-                    in_=w_dram[x][2 * P * u:2 * P * (u + 1), lo:lo + w_step[(x, g)]].rearrange(
-                        "(p e) c -> p e c", e=2),
-                )
+                    out=wq_raw[g][:, 2 * u:2 * u + 2, :],
+                    in_=wq2[2 * P * u:2 * P * (u + 1), K_PASS * g:K_PASS * (g + 1)].rearrange(
+                        "(p e) c -> p e c", e=2))
 
-        for what in LOADS:
-            if what[0] == "h":
-                load_h(what[1], what[2], what[3])
-            else:
-                load_w(what[1], what[2], what[3])
+        def load_wk():
+            for u in range(2):
+                nc.sync.dma_start(
+                    out=wk_raw[:, 2 * u:2 * u + 2, :],
+                    in_=wk2[2 * P * u:2 * P * (u + 1), :].rearrange("(p e) c -> p e c", e=2))
+
+        load_wq(0)
+        load_h(0, 0)
+        for g in range(1, G):
+            load_wq(g)
+        load_h(0, 1)
+        load_h(1, 0)
+        load_wk()
+        load_h(1, 1)
 
         make_identity(nc, ident[:])
         nc.vector.memset(warm_in[:], 0.0)
         nc.scalar.activation(out=warm_out[:], in_=warm_in[:], func=AF.Sigmoid)
 
-        def h_transposes(x, n, b0):
-            span = h_step[(x, n)]
+        def h_transposes(x, n, b0, span):
             xt = acc.tile([P, span, 2, P], F32, tag="acc", name="xt")
-            words = h_raw[(x, n, b0)][:].bitcast(F32)
+            words = h_raw[(x, n)][:].bitcast(F32)
             for b in range(span):
                 for u in range(2):
-                    lo = 2 * P * b + P * u
+                    lo = 2 * P * (b0 + b) + P * u
                     nc.tensor.transpose(xt[:, b, u, :], words[:, lo:lo + P], ident[:])
             return xt
 
-        def h_copy(copy, x, n, xt, hg, b0):
-            span = h_step[(x, n)]
+        def h_copy(copy, xt, hg, b0, span):
             dst = hg[:].bitcast(F32)[:, 2 * P * b0:2 * P * (b0 + span)]
             copy(out=dst.rearrange("p (b c u) -> p b c u", b=span, u=2),
                  in_=xt[:].rearrange("p b u c -> p b c u"))
 
-        def h_quant(x, n, hg, b0):
-            span = h_step[(x, n)]
+        def h_quant(x, n, hg, b0, span):
             cols = slice(P * b0, P * (b0 + span))
             nc.vector.quantize_mx(out=h_codes[x][n][:, cols].bitcast(FP8X4),
                                   scales=h_scales[x][n][:, cols],
                                   in_=hg[:, 4 * P * b0:4 * P * (b0 + span)])
 
         def w_regroup(copy, x, g, wg, m0, m1):
-            base = m0 - m0 % w_step[(x, g)]
+            src = wq_raw[g][:, :, m0:m1] if x == 0 else wk_raw[:, :, K_PASS * g + m0:K_PASS * g + m1]
             copy(out=wg[:, m0:m1, :].rearrange("p (c i) t -> p c t i", i=4),
-                 in_=w_raw[(x, g, base)][:, :, m0 - base:m1 - base].rearrange("p t (c i) -> p c t i", i=4))
+                 in_=src.rearrange("p t (c i) -> p c t i", i=4))
 
         def w_quant(x, g, wg, m0, m1):
             cols = slice(K_PASS * g + m0, K_PASS * g + m1)
@@ -139,12 +138,12 @@ def tile_complexchannelattn_pa_kernel(tc, hq, hk, wq2, wk2, out):
                                   in_=wg[:, m0:m1, :].rearrange("p m t -> p (m t)"))
 
         def prep_h(x, n):
-            xts = [h_transposes(x, n, b) for b in range(0, CB, 2)]
+            xts = [h_transposes(x, n, b, 2) for b in range(0, CB, 2)]
             hg = hgp.tile([P, 4 * C], BF16, name="hg", align_bytes=64)
             for b in range(0, CB, 2):
-                h_copy(nc.vector.tensor_copy, x, n, xts[b // 2], hg, b)
+                h_copy(nc.vector.tensor_copy, xts[b // 2], hg, b, 2)
             for b in range(0, CB, 2):
-                h_quant(x, n, hg, b)
+                h_quant(x, n, hg, b, 2)
 
         def prep_w(x, g):
             wg = wgp.tile([P, K_PASS, 4], BF16, name="wg", align_bytes=64)
@@ -209,25 +208,17 @@ def tile_complexchannelattn_pa_kernel(tc, hq, hk, wq2, wk2, out):
             nc.vector.reciprocal(out=rs[n][m][:], in_=sm[n][m][:])
             nc.vector.tensor_scalar(out=e_sb[n][m][:], in0=e_sb[n][m][:], scalar1=rs[n][m][:],
                                     scalar2=None, op0=ALU.mult)
-            nc.sync.dma_start(out=out[n, P * m:P * (m + 1), :], in_=e_sb[n][m][:])
+            nc.sync.dma_start(out=out[n].rearrange("(p b) c -> p b c", b=CB)[:, m, :], in_=e_sb[n][m][:])
 
         hg0 = hgp.tile([P, 4 * C], BF16, name="hg", align_bytes=64)
         wg0 = wgp.tile([P, K_PASS, 4], BF16, name="wg", align_bytes=64)
-        half = K_PASS // 2
-        def head_block(b, copy):
-            xt = h_transposes(0, 0, b)
-            h_copy(copy, 0, 0, xt, hg0, b)
-            h_quant(0, 0, hg0, b)
-
-        head_block(0, nc.scalar.copy)
-        w_regroup(nc.vector.tensor_copy, 0, 0, wg0, 0, half)
-        w_quant(0, 0, wg0, 0, half)
-        w_regroup(nc.vector.tensor_copy, 0, 0, wg0, half, half + P // 2 + HEAD_SPLIT)
-        w_regroup(nc.scalar.copy, 0, 0, wg0, half + P // 2 + HEAD_SPLIT, K_PASS)
-        w_quant(0, 0, wg0, half, K_PASS)
-        head_block(1, nc.scalar.copy)
-        head_block(2, nc.scalar.copy)
-        head_block(3, nc.vector.tensor_copy)
+        w_regroup(nc.vector.tensor_copy, 0, 0, wg0, 0, HEAD_SPLIT)
+        w_regroup(nc.scalar.copy, 0, 0, wg0, HEAD_SPLIT, K_PASS)
+        w_quant(0, 0, wg0, 0, K_PASS)
+        xt0 = [h_transposes(0, 0, b, 1) for b in range(CB)]
+        for b in range(CB):
+            h_copy(nc.vector.tensor_copy if b == 0 else nc.scalar.copy, xt0[b], hg0, b, 1)
+            h_quant(0, 0, hg0, b, 1)
         late_blocks = {}
 
         for u in range(UNITS):
@@ -269,7 +260,7 @@ def tile_complexchannelattn_pa_kernel(tc, hq, hk, wq2, wk2, out):
                 row_max(m + 2)
             nc.gpsimd.tensor_scalar(out=e_sb[0][m][:], in0=e_sb[0][m][:], scalar1=rs[0][m][:],
                                     scalar2=0.0, op0=ALU.mult, op1=ALU.add)
-            nc.sync.dma_start(out=out[0, P * m:P * (m + 1), :], in_=e_sb[0][m][:])
+            nc.sync.dma_start(out=out[0].rearrange("(p b) c -> p b c", b=CB)[:, m, :], in_=e_sb[0][m][:])
         for m in range(CB):
             nc.scalar.activation(out=e_sb[1][m][:], in_=s_ps[(1, m)][:], func=AF.Exp,
                                  bias=nb[1][m][:], scale=inv, accum_out=sm[1][m][:])

@@ -23,9 +23,13 @@ G = HW // K_PASS
 CB = C // P
 UNITS = 4 * G
 DRAIN = -1
-HEAD_SPLIT = 352
+HEAD_SPLIT = 64
 ORDER = [(0, 0, 0), (0, 0, 1), (0, 0, 2), (0, 0, 3), (1, 0, 0), (1, 0, 1), (0, 1, 0), (0, 1, 1),
          (0, 1, 2), (0, 1, 3), (1, 0, 2), (1, 0, 3), (1, 1, 0), (1, 1, 1), (1, 1, 2), (1, 1, 3)]
+LOADS = [("h", 0, 0, 0), ("w", 0, 0, 0), ("w", 0, 0, 256), ("h", 0, 0, 1), ("h", 0, 0, 2), ("h", 0, 0, 3),
+         ("w", 0, 1, 0), ("w", 0, 1, 256), ("w", 0, 2, 0), ("w", 0, 3, 0), ("h", 0, 1, 0), ("h", 0, 1, 2),
+         ("h", 1, 0, 0), ("h", 1, 0, 2), ("w", 1, 0, 0), ("w", 1, 1, 0), ("h", 1, 1, 0), ("h", 1, 1, 2),
+         ("w", 1, 2, 0), ("w", 1, 3, 0)]
 BEFORE = {1: [("w", 0, 2)], 2: [("w", 0, 3)], 3: [("h", 0, 1)], 4: [("h", 1, 0)],
           5: [("w", 1, 0)], 6: [("w", 1, 1), ("h", 1, 1)], 7: [("w", 1, 2)], 8: [("w", 1, 3)]}
 AFTER = {8: [0, 6], 9: [1, 7, 2, 8, 3, 9], 10: [4, 5, 10], 11: [11], 12: [DRAIN, 12], 13: [13], 14: [14]}
@@ -42,15 +46,17 @@ def tile_complexchannelattn_pa_kernel(tc, hq, hk, wq2, wk2, out):
         keep = ctx.enter_context(tc.tile_pool(name="keep", bufs=1))
         wgp = ctx.enter_context(tc.tile_pool(name="wgp", bufs=2))
         hgp = ctx.enter_context(tc.tile_pool(name="hgp", bufs=2))
-        agp = ctx.enter_context(tc.tile_pool(name="agp", bufs=8))
+        agp = ctx.enter_context(tc.tile_pool(name="agp", bufs=12))
         rot = ctx.enter_context(tc.psum_pool(name="rot", bufs=4))
         acc = ctx.enter_context(tc.psum_pool(name="acc", bufs=4))
         ctx.enter_context(tc.manual_schedule())
 
-        h_raw = {(x, n): keep.tile([P, CB * R], BF16, name="hraw%d%d" % (x, n))
-                 for x in range(2) for n in range(IMAGES)}
-        wq_raw = [keep.tile([P, 4, K_PASS], BF16, name="wqraw%d" % g) for g in range(G)]
-        wk_raw = keep.tile([P, 4, HW], BF16, name="wkraw")
+        h_step = {(x, n): (1 if (x, n) == (0, 0) else 2) for x in range(2) for n in range(IMAGES)}
+        h_raw = {(x, n, b): keep.tile([P, h_step[(x, n)] * R], BF16, name="hraw%d%d%d" % (x, n, b))
+                 for x in range(2) for n in range(IMAGES) for b in range(0, CB, h_step[(x, n)])}
+        w_step = {(x, g): (K_PASS // 2 if (x, g) in ((0, 0), (0, 1)) else K_PASS) for x in range(2) for g in range(G)}
+        w_raw = {(x, g, m): keep.tile([P, 4, w_step[(x, g)]], BF16, name="wraw%d%d%d" % (x, g, m))
+                 for x in range(2) for g in range(G) for m in range(0, K_PASS, w_step[(x, g)])}
         h_codes = [[keep.tile([P, C], U32, name="hc%d%d" % (x, n), align_bytes=64)
                     for n in range(IMAGES)] for x in range(2)]
         h_scales = [[keep.tile([P, C], U8, name="hs%d%d" % (x, n), align_bytes=64)
@@ -72,64 +78,59 @@ def tile_complexchannelattn_pa_kernel(tc, hq, hk, wq2, wk2, out):
         warm_in = keep.tile([P, 1], F32, name="warm_in")
         warm_out = keep.tile([P, 1], F32, name="warm_out")
 
-        def load_h(x, n):
-            if x == 0:
-                src = h_dram[x][n].rearrange("(p b) r -> p (b r)", b=CB)
-                nc.sync.dma_start(out=h_raw[(x, n)][:], in_=src)
+        def load_h(x, n, b):
+            span = h_step[(x, n)]
+            nc.sync.dma_start(
+                out=h_raw[(x, n, b)][:].rearrange("p (b r) -> p b r", b=span),
+                in_=h_dram[x][n, P * b:P * (b + span), :].rearrange("(b p) r -> p b r", p=P),
+            )
+
+        def load_w(x, g, m):
+            lo = K_PASS * g + m
+            for u in range(2):
+                nc.sync.dma_start(
+                    out=w_raw[(x, g, m)][:, 2 * u:2 * u + 2, :],
+                    in_=w_dram[x][2 * P * u:2 * P * (u + 1), lo:lo + w_step[(x, g)]].rearrange(
+                        "(p e) c -> p e c", e=2),
+                )
+
+        for what in LOADS:
+            if what[0] == "h":
+                load_h(what[1], what[2], what[3])
             else:
-                src = h_dram[x][n].rearrange("(b p) r -> p b r", p=P)
-                nc.sync.dma_start(out=h_raw[(x, n)][:].rearrange("p (b r) -> p b r", b=CB), in_=src)
-
-        def load_wq(g):
-            for u in range(2):
-                nc.sync.dma_start(
-                    out=wq_raw[g][:, 2 * u:2 * u + 2, :],
-                    in_=wq2[2 * P * u:2 * P * (u + 1), K_PASS * g:K_PASS * (g + 1)].rearrange(
-                        "(p e) c -> p e c", e=2))
-
-        def load_wk():
-            for u in range(2):
-                nc.sync.dma_start(
-                    out=wk_raw[:, 2 * u:2 * u + 2, :],
-                    in_=wk2[2 * P * u:2 * P * (u + 1), :].rearrange("(p e) c -> p e c", e=2))
-
-        load_wq(0)
-        load_h(0, 0)
-        for g in range(1, G):
-            load_wq(g)
-        load_h(0, 1)
-        load_h(1, 0)
-        load_wk()
-        load_h(1, 1)
+                load_w(what[1], what[2], what[3])
 
         make_identity(nc, ident[:])
         nc.vector.memset(warm_in[:], 0.0)
         nc.scalar.activation(out=warm_out[:], in_=warm_in[:], func=AF.Sigmoid)
 
-        def h_transposes(x, n, b0, span):
+        def h_transposes(x, n, b0):
+            span = h_step[(x, n)]
             xt = acc.tile([P, span, 2, P], F32, tag="acc", name="xt")
-            words = h_raw[(x, n)][:].bitcast(F32)
+            words = h_raw[(x, n, b0)][:].bitcast(F32)
             for b in range(span):
                 for u in range(2):
-                    lo = 2 * P * (b0 + b) + P * u
+                    lo = 2 * P * b + P * u
                     nc.tensor.transpose(xt[:, b, u, :], words[:, lo:lo + P], ident[:])
             return xt
 
-        def h_copy(copy, xt, hg, b0, span):
+        def h_copy(copy, x, n, xt, hg, b0):
+            span = h_step[(x, n)]
             dst = hg[:].bitcast(F32)[:, 2 * P * b0:2 * P * (b0 + span)]
             copy(out=dst.rearrange("p (b c u) -> p b c u", b=span, u=2),
                  in_=xt[:].rearrange("p b u c -> p b c u"))
 
-        def h_quant(x, n, hg, b0, span):
+        def h_quant(x, n, hg, b0):
+            span = h_step[(x, n)]
             cols = slice(P * b0, P * (b0 + span))
             nc.vector.quantize_mx(out=h_codes[x][n][:, cols].bitcast(FP8X4),
                                   scales=h_scales[x][n][:, cols],
                                   in_=hg[:, 4 * P * b0:4 * P * (b0 + span)])
 
         def w_regroup(copy, x, g, wg, m0, m1):
-            src = wq_raw[g][:, :, m0:m1] if x == 0 else wk_raw[:, :, K_PASS * g + m0:K_PASS * g + m1]
+            base = m0 - m0 % w_step[(x, g)]
             copy(out=wg[:, m0:m1, :].rearrange("p (c i) t -> p c t i", i=4),
-                 in_=src.rearrange("p t (c i) -> p c t i", i=4))
+                 in_=w_raw[(x, g, base)][:, :, m0 - base:m1 - base].rearrange("p t (c i) -> p c t i", i=4))
 
         def w_quant(x, g, wg, m0, m1):
             cols = slice(K_PASS * g + m0, K_PASS * g + m1)
@@ -138,12 +139,12 @@ def tile_complexchannelattn_pa_kernel(tc, hq, hk, wq2, wk2, out):
                                   in_=wg[:, m0:m1, :].rearrange("p m t -> p (m t)"))
 
         def prep_h(x, n):
-            xts = [h_transposes(x, n, b, 2) for b in range(0, CB, 2)]
+            xts = [h_transposes(x, n, b) for b in range(0, CB, 2)]
             hg = hgp.tile([P, 4 * C], BF16, name="hg", align_bytes=64)
             for b in range(0, CB, 2):
-                h_copy(nc.vector.tensor_copy, xts[b // 2], hg, b, 2)
+                h_copy(nc.vector.tensor_copy, x, n, xts[b // 2], hg, b)
             for b in range(0, CB, 2):
-                h_quant(x, n, hg, b, 2)
+                h_quant(x, n, hg, b)
 
         def prep_w(x, g):
             wg = wgp.tile([P, K_PASS, 4], BF16, name="wg", align_bytes=64)
@@ -208,17 +209,25 @@ def tile_complexchannelattn_pa_kernel(tc, hq, hk, wq2, wk2, out):
             nc.vector.reciprocal(out=rs[n][m][:], in_=sm[n][m][:])
             nc.vector.tensor_scalar(out=e_sb[n][m][:], in0=e_sb[n][m][:], scalar1=rs[n][m][:],
                                     scalar2=None, op0=ALU.mult)
-            nc.sync.dma_start(out=out[n].rearrange("(p b) c -> p b c", b=CB)[:, m, :], in_=e_sb[n][m][:])
+            nc.sync.dma_start(out=out[n, P * m:P * (m + 1), :], in_=e_sb[n][m][:])
 
         hg0 = hgp.tile([P, 4 * C], BF16, name="hg", align_bytes=64)
         wg0 = wgp.tile([P, K_PASS, 4], BF16, name="wg", align_bytes=64)
-        w_regroup(nc.vector.tensor_copy, 0, 0, wg0, 0, HEAD_SPLIT)
-        w_regroup(nc.scalar.copy, 0, 0, wg0, HEAD_SPLIT, K_PASS)
-        w_quant(0, 0, wg0, 0, K_PASS)
-        xt0 = [h_transposes(0, 0, b, 1) for b in range(CB)]
-        for b in range(CB):
-            h_copy(nc.vector.tensor_copy if b == 0 else nc.scalar.copy, xt0[b], hg0, b, 1)
-            h_quant(0, 0, hg0, b, 1)
+        half = K_PASS // 2
+        def head_block(b, copy):
+            xt = h_transposes(0, 0, b)
+            h_copy(copy, 0, 0, xt, hg0, b)
+            h_quant(0, 0, hg0, b)
+
+        head_block(0, nc.scalar.copy)
+        w_regroup(nc.vector.tensor_copy, 0, 0, wg0, 0, half)
+        w_quant(0, 0, wg0, 0, half)
+        w_regroup(nc.vector.tensor_copy, 0, 0, wg0, half, half + P // 2 + HEAD_SPLIT)
+        w_regroup(nc.scalar.copy, 0, 0, wg0, half + P // 2 + HEAD_SPLIT, K_PASS)
+        w_quant(0, 0, wg0, half, K_PASS)
+        head_block(1, nc.scalar.copy)
+        head_block(2, nc.scalar.copy)
+        head_block(3, nc.vector.tensor_copy)
         late_blocks = {}
 
         for u in range(UNITS):
@@ -260,7 +269,7 @@ def tile_complexchannelattn_pa_kernel(tc, hq, hk, wq2, wk2, out):
                 row_max(m + 2)
             nc.gpsimd.tensor_scalar(out=e_sb[0][m][:], in0=e_sb[0][m][:], scalar1=rs[0][m][:],
                                     scalar2=0.0, op0=ALU.mult, op1=ALU.add)
-            nc.sync.dma_start(out=out[0].rearrange("(p b) c -> p b c", b=CB)[:, m, :], in_=e_sb[0][m][:])
+            nc.sync.dma_start(out=out[0, P * m:P * (m + 1), :], in_=e_sb[0][m][:])
         for m in range(CB):
             nc.scalar.activation(out=e_sb[1][m][:], in_=s_ps[(1, m)][:], func=AF.Exp,
                                  bias=nb[1][m][:], scale=inv, accum_out=sm[1][m][:])

@@ -9,31 +9,23 @@ BF16 = mybir.dt.bfloat16
 U32 = mybir.dt.uint32
 U8 = mybir.dt.uint8
 FP8X4 = mybir.dt.float8_e4m3fn_x4
-AF = mybir.ActivationFunctionType
+SIGMOID = mybir.ActivationFunctionType.Sigmoid
 ALU = mybir.AluOpType
-AX = mybir.AxisListType
 
 P = 128
+PACK = 4
+K_PASS = P * PACK
 IMAGES = 2
 C = 512
 R = 512
 HW = 2048
-K_PASS = 512
-G = HW // K_PASS
-CB = C // P
-UNITS = 4 * G
-DRAIN = -1
-HEAD_SPLIT = 64
-ORDER = [(0, 0, 0), (0, 0, 1), (0, 0, 2), (0, 0, 3), (1, 0, 0), (1, 0, 1), (0, 1, 0), (0, 1, 1),
-         (0, 1, 2), (0, 1, 3), (1, 0, 2), (1, 0, 3), (1, 1, 0), (1, 1, 1), (1, 1, 2), (1, 1, 3)]
-LOADS = [("h", 0, 0, 0), ("w", 0, 0, 0), ("w", 0, 0, 256), ("h", 0, 0, 1), ("h", 0, 0, 2), ("h", 0, 0, 3),
-         ("w", 0, 1, 0), ("w", 0, 1, 256), ("w", 0, 2, 0), ("w", 0, 3, 0), ("h", 0, 1, 0), ("h", 0, 1, 2),
-         ("h", 1, 0, 0), ("h", 1, 0, 2), ("w", 1, 0, 0), ("w", 1, 1, 0), ("h", 1, 1, 0), ("h", 1, 1, 2),
-         ("w", 1, 2, 0), ("w", 1, 3, 0)]
-BEFORE = {1: [("w", 0, 2)], 2: [("w", 0, 3)], 3: [("h", 0, 1)], 4: [("h", 1, 0)],
-          5: [("w", 1, 0)], 6: [("w", 1, 1), ("h", 1, 1)], 7: [("w", 1, 2)], 8: [("w", 1, 3)]}
-AFTER = {8: [0, 6], 9: [1, 7, 2, 8, 3, 9], 10: [4, 5, 10], 11: [11], 12: [DRAIN, 12], 13: [13], 14: [14]}
-SCORES = {9: [(0, 0)], 10: [(0, 1)], 11: [(0, 2)], 12: [(0, 3)], 14: [(1, 0)], 15: [(1, 1), (1, 2)]}
+PASSES = HW // K_PASS
+BLOCKS = C // P
+Q = 0
+K = 1
+UNITS = 2 * IMAGES * PASSES
+SCORE_LAG = 2
+SHIFT = 24.0
 FLOPS = 2 * 2 * IMAGES * C * R * HW + 2 * IMAGES * C * C * HW
 
 
@@ -42,235 +34,247 @@ def tile_complexchannelattn_pa_kernel(tc, hq, hk, wq2, wk2, out):
     h_dram = (hq, hk)
     w_dram = (wq2, wk2)
     inv = 1.0 / math.sqrt(C)
+    half = K_PASS // 2
+
+    def unit_of(u):
+        return u // (IMAGES * PASSES), (u // PASSES) % IMAGES, u % PASSES
+
+    operands = []
+    for u in range(UNITS):
+        side, n, g = unit_of(u)
+        for operand in (("h", side, n), ("w", side, g)):
+            if operand not in operands:
+                operands.append(operand)
+
+    def h_step(side, n):
+        return 1 if (side, n) == (Q, 0) else 2
+
+    def w_step(side, g):
+        return half if side == Q and g < 2 else K_PASS
+
     with ExitStack() as ctx:
         keep = ctx.enter_context(tc.tile_pool(name="keep", bufs=1))
-        wgp = ctx.enter_context(tc.tile_pool(name="wgp", bufs=2))
-        hgp = ctx.enter_context(tc.tile_pool(name="hgp", bufs=2))
-        agp = ctx.enter_context(tc.tile_pool(name="agp", bufs=12))
-        rot = ctx.enter_context(tc.psum_pool(name="rot", bufs=4))
-        acc = ctx.enter_context(tc.psum_pool(name="acc", bufs=4))
+        w_stage = ctx.enter_context(tc.tile_pool(name="w_stage", bufs=2))
+        h_stage = ctx.enter_context(tc.tile_pool(name="h_stage", bufs=2))
+        a_stage = ctx.enter_context(tc.tile_pool(name="a_stage", bufs=2 * PASSES))
+        z_banks = ctx.enter_context(tc.psum_pool(name="z_banks", bufs=4))
+        s_banks = ctx.enter_context(tc.psum_pool(name="s_banks", bufs=4))
         ctx.enter_context(tc.manual_schedule())
 
-        h_step = {(x, n): (1 if (x, n) == (0, 0) else 2) for x in range(2) for n in range(IMAGES)}
-        h_raw = {(x, n, b): keep.tile([P, h_step[(x, n)] * R], BF16, name="hraw%d%d%d" % (x, n, b))
-                 for x in range(2) for n in range(IMAGES) for b in range(0, CB, h_step[(x, n)])}
-        w_step = {(x, g): (K_PASS // 2 if (x, g) in ((0, 0), (0, 1)) else K_PASS) for x in range(2) for g in range(G)}
-        w_raw = {(x, g, m): keep.tile([P, 4, w_step[(x, g)]], BF16, name="wraw%d%d%d" % (x, g, m))
-                 for x in range(2) for g in range(G) for m in range(0, K_PASS, w_step[(x, g)])}
-        h_codes = [[keep.tile([P, C], U32, name="hc%d%d" % (x, n), align_bytes=64)
-                    for n in range(IMAGES)] for x in range(2)]
-        h_scales = [[keep.tile([P, C], U8, name="hs%d%d" % (x, n), align_bytes=64)
-                     for n in range(IMAGES)] for x in range(2)]
-        w_codes = [keep.tile([P, HW], U32, name="wc%d" % x, align_bytes=64) for x in range(2)]
-        w_scales = [keep.tile([P, HW], U8, name="ws%d" % x, align_bytes=64) for x in range(2)]
-        a_codes = [[keep.tile([P, G, C], U32, name="ac%d%d" % (x, n), align_bytes=64)
-                    for n in range(IMAGES)] for x in range(2)]
-        a_scales = [[keep.tile([P, G, C], U8, name="as%d%d" % (x, n), align_bytes=64)
-                     for n in range(IMAGES)] for x in range(2)]
-        s_sb = [keep.tile([P, C], F32, name="ssb%d" % m) for m in range(CB)]
-        e_sb = [[keep.tile([P, C], F32, name="e%d%d" % (n, m)) for m in range(CB)]
-                for n in range(IMAGES)]
-        mx = [[keep.tile([P, 1], F32, name="mx%d%d" % (n, m)) for m in range(CB)] for n in range(IMAGES)]
-        nb = [[keep.tile([P, 1], F32, name="nb%d%d" % (n, m)) for m in range(CB)] for n in range(IMAGES)]
-        sm = [[keep.tile([P, 1], F32, name="sm%d%d" % (n, m)) for m in range(CB)] for n in range(IMAGES)]
-        rs = [[keep.tile([P, 1], F32, name="rs%d%d" % (n, m)) for m in range(CB)] for n in range(IMAGES)]
+        h_raw = {(side, n, b): keep.tile([P, h_step(side, n) * R], BF16, name="h_raw%d%d%d" % (side, n, b))
+                 for side in (Q, K) for n in range(IMAGES) for b in range(0, BLOCKS, h_step(side, n))}
+        w_raw = {(side, g, m): keep.tile([P, PACK, w_step(side, g)], BF16, name="w_raw%d%d%d" % (side, g, m))
+                 for side in (Q, K) for g in range(PASSES) for m in range(0, K_PASS, w_step(side, g))}
+        h_codes = [[keep.tile([P, C], U32, name="h_codes%d%d" % (side, n), align_bytes=64)
+                    for n in range(IMAGES)] for side in (Q, K)]
+        h_scales = [[keep.tile([P, C], U8, name="h_scales%d%d" % (side, n), align_bytes=64)
+                     for n in range(IMAGES)] for side in (Q, K)]
+        w_codes = [keep.tile([P, HW], U32, name="w_codes%d" % side, align_bytes=64) for side in (Q, K)]
+        w_scales = [keep.tile([P, HW], U8, name="w_scales%d" % side, align_bytes=64) for side in (Q, K)]
+        a_codes = [[keep.tile([P, PASSES, C], U32, name="a_codes%d%d" % (side, n), align_bytes=64)
+                    for n in range(IMAGES)] for side in (Q, K)]
+        a_scales = [[keep.tile([P, PASSES, C], U8, name="a_scales%d%d" % (side, n), align_bytes=64)
+                     for n in range(IMAGES)] for side in (Q, K)]
+        s_parked = [keep.tile([P, C], F32, name="s_parked%d" % m) for m in range(BLOCKS)]
+        weights = [[keep.tile([P, C], F32, name="weights%d%d" % (n, m)) for m in range(BLOCKS)]
+                   for n in range(IMAGES)]
+
+        def column(name):
+            return [[keep.tile([P, 1], F32, name="%s%d%d" % (name, n, m)) for m in range(BLOCKS)]
+                    for n in range(IMAGES)]
+
+        row_max, bias, row_sum, scale = column("row_max"), column("bias"), column("row_sum"), column("scale")
         ident = keep.tile([P, P], F32, name="ident")
         warm_in = keep.tile([P, 1], F32, name="warm_in")
         warm_out = keep.tile([P, 1], F32, name="warm_out")
 
-        def load_h(x, n, b):
-            span = h_step[(x, n)]
+        def load_h(side, n, b):
+            blocks = h_step(side, n)
             nc.sync.dma_start(
-                out=h_raw[(x, n, b)][:].rearrange("p (b r) -> p b r", b=span),
-                in_=h_dram[x][n, P * b:P * (b + span), :].rearrange("(b p) r -> p b r", p=P),
-            )
+                out=h_raw[(side, n, b)][:].rearrange("p (b r) -> p b r", b=blocks),
+                in_=h_dram[side][n, P * b:P * (b + blocks), :].rearrange("(b p) r -> p b r", p=P))
 
-        def load_w(x, g, m):
+        def load_w(side, g, m):
             lo = K_PASS * g + m
             for u in range(2):
                 nc.sync.dma_start(
-                    out=w_raw[(x, g, m)][:, 2 * u:2 * u + 2, :],
-                    in_=w_dram[x][2 * P * u:2 * P * (u + 1), lo:lo + w_step[(x, g)]].rearrange(
-                        "(p e) c -> p e c", e=2),
-                )
+                    out=w_raw[(side, g, m)][:, 2 * u:2 * u + 2, :],
+                    in_=w_dram[side][2 * P * u:2 * P * (u + 1), lo:lo + w_step(side, g)].rearrange(
+                        "(p e) c -> p e c", e=2))
 
-        for what in LOADS:
-            if what[0] == "h":
-                load_h(what[1], what[2], what[3])
+        load_h(Q, 0, 0)
+        for m in range(0, K_PASS, half):
+            load_w(Q, 0, m)
+        for b in range(1, BLOCKS):
+            load_h(Q, 0, b)
+        for kind, side, i in operands[2:]:
+            if kind == "h":
+                for b in range(0, BLOCKS, h_step(side, i)):
+                    load_h(side, i, b)
             else:
-                load_w(what[1], what[2], what[3])
+                for m in range(0, K_PASS, w_step(side, i)):
+                    load_w(side, i, m)
 
         make_identity(nc, ident[:])
         nc.vector.memset(warm_in[:], 0.0)
-        nc.scalar.activation(out=warm_out[:], in_=warm_in[:], func=AF.Sigmoid)
+        nc.scalar.activation(out=warm_out[:], in_=warm_in[:], func=SIGMOID)
 
-        def h_transposes(x, n, b0):
-            span = h_step[(x, n)]
-            xt = acc.tile([P, span, 2, P], F32, tag="acc", name="xt")
-            words = h_raw[(x, n, b0)][:].bitcast(F32)
-            for b in range(span):
+        def h_transposes(side, n, b0):
+            blocks = h_step(side, n)
+            planes = s_banks.tile([P, blocks, 2, P], F32, tag="s_banks", name="planes")
+            words = h_raw[(side, n, b0)][:].bitcast(F32)
+            for b in range(blocks):
                 for u in range(2):
                     lo = 2 * P * b + P * u
-                    nc.tensor.transpose(xt[:, b, u, :], words[:, lo:lo + P], ident[:])
-            return xt
+                    nc.tensor.transpose(planes[:, b, u, :], words[:, lo:lo + P], ident[:])
+            return planes
 
-        def h_copy(copy, x, n, xt, hg, b0):
-            span = h_step[(x, n)]
-            dst = hg[:].bitcast(F32)[:, 2 * P * b0:2 * P * (b0 + span)]
-            copy(out=dst.rearrange("p (b c u) -> p b c u", b=span, u=2),
-                 in_=xt[:].rearrange("p b u c -> p b c u"))
+        def h_copy(copy, side, n, planes, grouped, b0):
+            blocks = h_step(side, n)
+            dst = grouped[:].bitcast(F32)[:, 2 * P * b0:2 * P * (b0 + blocks)]
+            copy(out=dst.rearrange("p (b c u) -> p b c u", b=blocks, u=2),
+                 in_=planes[:].rearrange("p b u c -> p b c u"))
 
-        def h_quant(x, n, hg, b0):
-            span = h_step[(x, n)]
-            cols = slice(P * b0, P * (b0 + span))
-            nc.vector.quantize_mx(out=h_codes[x][n][:, cols].bitcast(FP8X4),
-                                  scales=h_scales[x][n][:, cols],
-                                  in_=hg[:, 4 * P * b0:4 * P * (b0 + span)])
+        def h_quantise(side, n, grouped, b0):
+            c0, c1 = P * b0, P * (b0 + h_step(side, n))
+            nc.vector.quantize_mx(out=h_codes[side][n][:, c0:c1].bitcast(FP8X4),
+                                  scales=h_scales[side][n][:, c0:c1],
+                                  in_=grouped[:, PACK * c0:PACK * c1])
 
-        def w_regroup(copy, x, g, wg, m0, m1):
-            base = m0 - m0 % w_step[(x, g)]
-            copy(out=wg[:, m0:m1, :].rearrange("p (c i) t -> p c t i", i=4),
-                 in_=w_raw[(x, g, base)][:, :, m0 - base:m1 - base].rearrange("p t (c i) -> p c t i", i=4))
+        def w_regroup(copy, side, g, grouped, m0, m1):
+            base = m0 - m0 % w_step(side, g)
+            copy(out=grouped[:, m0:m1, :].rearrange("p (c i) t -> p c t i", i=4),
+                 in_=w_raw[(side, g, base)][:, :, m0 - base:m1 - base].rearrange("p t (c i) -> p c t i", i=4))
 
-        def w_quant(x, g, wg, m0, m1):
+        def w_quantise(side, g, grouped, m0, m1):
             cols = slice(K_PASS * g + m0, K_PASS * g + m1)
-            nc.vector.quantize_mx(out=w_codes[x][:, cols].bitcast(FP8X4),
-                                  scales=w_scales[x][:, cols],
-                                  in_=wg[:, m0:m1, :].rearrange("p m t -> p (m t)"))
+            nc.vector.quantize_mx(out=w_codes[side][:, cols].bitcast(FP8X4),
+                                  scales=w_scales[side][:, cols],
+                                  in_=grouped[:, m0:m1, :].rearrange("p m t -> p (m t)"))
 
-        def prep_h(x, n):
-            xts = [h_transposes(x, n, b) for b in range(0, CB, 2)]
-            hg = hgp.tile([P, 4 * C], BF16, name="hg", align_bytes=64)
-            for b in range(0, CB, 2):
-                h_copy(nc.vector.tensor_copy, x, n, xts[b // 2], hg, b)
-            for b in range(0, CB, 2):
-                h_quant(x, n, hg, b)
+        def prepare(kind, side, i):
+            if kind == "h":
+                starts = range(0, BLOCKS, h_step(side, i))
+                planes = [h_transposes(side, i, b) for b in starts]
+                grouped = h_stage.tile([P, PACK * C], BF16, name="h_grouped", align_bytes=64)
+                for b in starts:
+                    h_copy(nc.vector.tensor_copy, side, i, planes[b // 2], grouped, b)
+                for b in starts:
+                    h_quantise(side, i, grouped, b)
+            else:
+                grouped = w_stage.tile([P, K_PASS, PACK], BF16, name="w_grouped", align_bytes=64)
+                for m in (0, half):
+                    w_regroup(nc.vector.tensor_copy, side, i, grouped, m, m + half)
+                for m in (0, half):
+                    w_quantise(side, i, grouped, m, m + half)
 
-        def prep_w(x, g):
-            wg = wgp.tile([P, K_PASS, 4], BF16, name="wg", align_bytes=64)
-            half = K_PASS // 2
-            for f in range(2):
-                w_regroup(nc.vector.tensor_copy, x, g, wg, half * f, half * (f + 1))
-            for f in range(2):
-                w_quant(x, g, wg, half * f, half * (f + 1))
+        squashed = {}
 
-        def a_quant(x, n, g, ag, c0, c1):
-            nc.vector.quantize_mx(out=a_codes[x][n][:, g, c0:c1].bitcast(FP8X4),
-                                  scales=a_scales[x][n][:, g, c0:c1],
-                                  in_=ag[:, 4 * c0:4 * c1])
+        def a_quantise(u, c0, c1):
+            side, n, g = unit_of(u)
+            nc.vector.quantize_mx(out=a_codes[side][n][:, g, c0:c1].bitcast(FP8X4),
+                                  scales=a_scales[side][n][:, g, c0:c1],
+                                  in_=squashed[u][:, PACK * c0:PACK * c1])
 
-        def unit_of(u):
-            return ORDER[u]
-
-        ags = {}
-
-        def run_unit(u, quantise_each_bank, before_bank):
-            n, x, g = unit_of(u)
-            ag = agp.tile([P, 4 * C], BF16, name="ag", align_bytes=64)
-            ags[u] = ag
-            for cb in range(CB):
-                if cb in before_bank:
-                    before_bank[cb]()
-                bank = rot.tile([P, 4, P], F32, tag="rot", name="bank")
-                for j in range(4):
-                    wcols = slice(K_PASS * g + P * j, K_PASS * g + P * (j + 1))
-                    hcols = slice(P * cb, P * (cb + 1))
-                    nc.tensor.matmul_mx(out=bank[:, j, :],
-                                        lhsT=w_codes[x][:, wcols].bitcast(FP8X4),
-                                        lhsT_scale=w_scales[x][:, wcols],
-                                        rhs=h_codes[x][n][:, hcols].bitcast(FP8X4),
-                                        rhs_scale=h_scales[x][n][:, hcols],
+        def run_unit(u):
+            side, n, g = unit_of(u)
+            squashed[u] = a_stage.tile([P, PACK * C], BF16, name="squashed", align_bytes=64)
+            for b in range(BLOCKS):
+                z = z_banks.tile([P, PACK, P], F32, tag="z_banks", name="z")
+                channels = slice(P * b, P * (b + 1))
+                for j in range(PACK):
+                    positions = slice(K_PASS * g + P * j, K_PASS * g + P * (j + 1))
+                    nc.tensor.matmul_mx(out=z[:, j, :],
+                                        lhsT=w_codes[side][:, positions].bitcast(FP8X4),
+                                        lhsT_scale=w_scales[side][:, positions],
+                                        rhs=h_codes[side][n][:, channels].bitcast(FP8X4),
+                                        rhs_scale=h_scales[side][n][:, channels],
                                         start=True, stop=True)
                 nc.scalar.activation(
-                    out=ag[:, 4 * P * cb:4 * P * (cb + 1)].rearrange("p (c j) -> p c j", j=4),
-                    in_=bank[:].rearrange("p j c -> p c j"), func=AF.Sigmoid)
-                if quantise_each_bank:
-                    a_quant(x, n, g, ag, P * cb, P * (cb + 1))
+                    out=squashed[u][:, PACK * P * b:PACK * P * (b + 1)].rearrange("p (c j) -> p c j", j=PACK),
+                    in_=z[:].rearrange("p j c -> p c j"), func=SIGMOID)
+                if u == UNITS - 1:
+                    a_quantise(u, P * b, P * (b + 1))
 
-        def quantise_unit(u):
-            n, x, g = unit_of(u)
-            a_quant(x, n, g, ags[u], 0, C)
-
-        s_ps = {}
+        s_open = {}
 
         def scores(n, g):
-            for m in range(CB):
+            for m in range(BLOCKS):
                 if g == 0:
-                    s_ps[(n, m)] = acc.tile([P, C], F32, tag="acc", name="s")
-                mcols = slice(P * m, P * (m + 1))
-                nc.tensor.matmul_mx(out=s_ps[(n, m)][:],
-                                    lhsT=a_codes[0][n][:, g, mcols].bitcast(FP8X4),
-                                    lhsT_scale=a_scales[0][n][:, g, mcols],
-                                    rhs=a_codes[1][n][:, g, :].bitcast(FP8X4),
-                                    rhs_scale=a_scales[1][n][:, g, :],
-                                    start=(g == 0), stop=(g == G - 1))
+                    s_open[(n, m)] = s_banks.tile([P, C], F32, tag="s_banks", name="s")
+                rows = slice(P * m, P * (m + 1))
+                nc.tensor.matmul_mx(out=s_open[(n, m)][:],
+                                    lhsT=a_codes[Q][n][:, g, rows].bitcast(FP8X4),
+                                    lhsT_scale=a_scales[Q][n][:, g, rows],
+                                    rhs=a_codes[K][n][:, g, :].bitcast(FP8X4),
+                                    rhs_scale=a_scales[K][n][:, g, :],
+                                    start=(g == 0), stop=(g == PASSES - 1))
 
-        def finish(n, m):
-            nc.vector.reciprocal(out=rs[n][m][:], in_=sm[n][m][:])
-            nc.vector.tensor_scalar(out=e_sb[n][m][:], in0=e_sb[n][m][:], scalar1=rs[n][m][:],
-                                    scalar2=None, op0=ALU.mult)
-            nc.sync.dma_start(out=out[n, P * m:P * (m + 1), :], in_=e_sb[n][m][:])
+        def park(m):
+            nc.vector.tensor_scalar(out=s_parked[m][:], in0=s_open[(0, m)][:], scalar1=inv, scalar2=None,
+                                    op0=ALU.mult, op1=ALU.max, accum_out=row_max[0][m][:])
+            nc.vector.tensor_scalar(out=bias[0][m][:], in0=row_max[0][m][:], scalar1=-1.0, scalar2=-SHIFT,
+                                    op0=ALU.mult, op1=ALU.add)
 
-        hg0 = hgp.tile([P, 4 * C], BF16, name="hg", align_bytes=64)
-        wg0 = wgp.tile([P, K_PASS, 4], BF16, name="wg", align_bytes=64)
-        half = K_PASS // 2
-        def head_block(b, copy):
-            xt = h_transposes(0, 0, b)
-            h_copy(copy, 0, 0, xt, hg0, b)
-            h_quant(0, 0, hg0, b)
+        def maximum(m):
+            nc.vector.tensor_reduce(out=row_max[1][m][:], in_=s_open[(1, m)][:],
+                                    axis=mybir.AxisListType.X, op=ALU.max)
+            nc.vector.tensor_scalar(out=bias[1][m][:], in0=row_max[1][m][:], scalar1=-inv, scalar2=-SHIFT,
+                                    op0=ALU.mult, op1=ALU.add)
 
-        head_block(0, nc.scalar.copy)
-        w_regroup(nc.vector.tensor_copy, 0, 0, wg0, 0, half)
-        w_quant(0, 0, wg0, 0, half)
-        w_regroup(nc.vector.tensor_copy, 0, 0, wg0, half, half + P // 2 + HEAD_SPLIT)
-        w_regroup(nc.scalar.copy, 0, 0, wg0, half + P // 2 + HEAD_SPLIT, K_PASS)
-        w_quant(0, 0, wg0, half, K_PASS)
-        head_block(1, nc.scalar.copy)
-        head_block(2, nc.scalar.copy)
-        head_block(3, nc.vector.tensor_copy)
-        late_blocks = {}
+        def exponentials(n, m):
+            nc.scalar.activation(out=weights[n][m][:], in_=(s_parked[m] if n == 0 else s_open[(n, m)])[:],
+                                 func=SIGMOID, bias=bias[n][m][:], scale=(1.0 if n == 0 else inv),
+                                 accum_out=row_sum[n][m][:])
+
+        def normalise(engine, n, m):
+            nc.vector.reciprocal(out=scale[n][m][:], in_=row_sum[n][m][:])
+            engine.tensor_scalar(out=weights[n][m][:], in0=weights[n][m][:], scalar1=scale[n][m][:],
+                                 scalar2=0.0, op0=ALU.mult, op1=ALU.add)
+            nc.sync.dma_start(out=out[n, P * m:P * (m + 1), :], in_=weights[n][m][:])
+
+        h_grouped0 = h_stage.tile([P, PACK * C], BF16, name="h_grouped", align_bytes=64)
+        w_grouped0 = w_stage.tile([P, K_PASS, PACK], BF16, name="w_grouped", align_bytes=64)
+
+        def first_block(b, copy):
+            planes = h_transposes(Q, 0, b)
+            h_copy(copy, Q, 0, planes, h_grouped0, b)
+            h_quantise(Q, 0, h_grouped0, b)
+
+        first_block(0, nc.scalar.copy)
+        w_regroup(nc.vector.tensor_copy, Q, 0, w_grouped0, 0, half)
+        w_quantise(Q, 0, w_grouped0, 0, half)
+        w_regroup(nc.vector.tensor_copy, Q, 0, w_grouped0, half, half + P)
+        w_regroup(nc.scalar.copy, Q, 0, w_grouped0, half + P, K_PASS)
+        w_quantise(Q, 0, w_grouped0, half, K_PASS)
+        for b in range(1, BLOCKS):
+            first_block(b, nc.scalar.copy if b < BLOCKS - 1 else nc.vector.tensor_copy)
 
         for u in range(UNITS):
-            for kind, x, i in BEFORE.get(u, []):
-                if kind == "w":
-                    prep_w(x, i)
-                else:
-                    prep_h(x, i)
-            run_unit(u, u == UNITS - 1, late_blocks if u == 0 else {})
-            if u == 0:
-                prep_w(0, 1)
-            for n, g in SCORES.get(u, []):
-                scores(n, g)
-            for v in AFTER.get(u, []):
-                if v == DRAIN:
-                    for m in range(CB):
-                        nc.vector.tensor_scalar(out=s_sb[m][:], in0=s_ps[(0, m)][:], scalar1=inv,
-                                                scalar2=None, op0=ALU.mult, op1=ALU.max,
-                                                accum_out=mx[0][m][:])
-                        nc.vector.tensor_scalar(out=nb[0][m][:], in0=mx[0][m][:], scalar1=-1.0,
-                                                scalar2=None, op0=ALU.mult)
-                else:
-                    quantise_unit(v)
+            side, n, g = unit_of(u)
+            if u + 2 < len(operands):
+                prepare(*operands[u + 2])
+            run_unit(u)
+            if u >= SCORE_LAG and unit_of(u - SCORE_LAG)[:2] == (K, 0):
+                scores(0, unit_of(u - SCORE_LAG)[2])
+                if unit_of(u - SCORE_LAG)[2] == PASSES - 1:
+                    for m in range(BLOCKS):
+                        park(m)
+            if PASSES <= u < PASSES + IMAGES * PASSES:
+                a_quantise(u - PASSES, 0, C)
+            if side == K and u < UNITS - 1:
+                a_quantise(u, 0, C)
 
-        def row_max(m):
-            nc.vector.tensor_reduce(out=mx[1][m][:], in_=s_ps[(1, m)][:], axis=AX.X, op=ALU.max)
-            nc.vector.tensor_scalar(out=nb[1][m][:], in0=mx[1][m][:], scalar1=-inv,
-                                    scalar2=None, op0=ALU.mult)
-
-        scores(1, G - 1)
-        row_max(0)
-        row_max(1)
-        for m in range(CB):
-            nc.scalar.activation(out=e_sb[0][m][:], in_=s_sb[m][:], func=AF.Exp,
-                                 bias=nb[0][m][:], scale=1.0, accum_out=sm[0][m][:])
-        for m in range(CB):
-            nc.vector.reciprocal(out=rs[0][m][:], in_=sm[0][m][:])
-            if m + 2 < CB:
-                row_max(m + 2)
-            nc.gpsimd.tensor_scalar(out=e_sb[0][m][:], in0=e_sb[0][m][:], scalar1=rs[0][m][:],
-                                    scalar2=0.0, op0=ALU.mult, op1=ALU.add)
-            nc.sync.dma_start(out=out[0, P * m:P * (m + 1), :], in_=e_sb[0][m][:])
-        for m in range(CB):
-            nc.scalar.activation(out=e_sb[1][m][:], in_=s_ps[(1, m)][:], func=AF.Exp,
-                                 bias=nb[1][m][:], scale=inv, accum_out=sm[1][m][:])
-            finish(1, m)
+        for g in range(PASSES):
+            scores(1, g)
+        for m in range(BLOCKS):
+            exponentials(0, m)
+        for m in range(BLOCKS // 2):
+            normalise(nc.vector, 0, m)
+        for m in range(BLOCKS):
+            if m < BLOCKS // 2:
+                normalise(nc.gpsimd, 0, m + BLOCKS // 2)
+            maximum(m)
+        for m in range(BLOCKS):
+            exponentials(1, m)
+            normalise(nc.vector, 1, m)

@@ -20,7 +20,8 @@ C = 512
 R = 512
 HW = 2048
 PASSES = HW // K_PASS
-BLOCKS = C // P
+HALF_CHUNK = K_PASS // 2
+SLABS = C // P
 Q = 0
 K = 1
 UNITS = 2 * IMAGES * PASSES
@@ -34,14 +35,13 @@ def tile_complexchannelattn_pa_kernel(tc, hq, hk, wq2, wk2, out):
     h_dram = (hq, hk)
     w_dram = (wq2, wk2)
     inv = 1.0 / math.sqrt(C)
-    half = K_PASS // 2
 
-    def unit_of(u):
-        return u // (IMAGES * PASSES), (u // PASSES) % IMAGES, u % PASSES
+    def unit_of(unit):
+        return unit // (IMAGES * PASSES), (unit // PASSES) % IMAGES, unit % PASSES
 
     operands = []
-    for u in range(UNITS):
-        side, n, g = unit_of(u)
+    for unit in range(UNITS):
+        side, n, g = unit_of(unit)
         for operand in (("h", side, n), ("w", side, g)):
             if operand not in operands:
                 operands.append(operand)
@@ -50,7 +50,7 @@ def tile_complexchannelattn_pa_kernel(tc, hq, hk, wq2, wk2, out):
         return 1 if (side, n) == (Q, 0) else 2
 
     def w_step(side, g):
-        return half if side == Q and g < 2 else K_PASS
+        return HALF_CHUNK if side == Q and g < 2 else K_PASS
 
     with ExitStack() as ctx:
         keep = ctx.enter_context(tc.tile_pool(name="keep", bufs=1))
@@ -62,9 +62,10 @@ def tile_complexchannelattn_pa_kernel(tc, hq, hk, wq2, wk2, out):
         ctx.enter_context(tc.manual_schedule())
 
         h_raw = {(side, n, b): keep.tile([P, h_step(side, n) * R], BF16, name="h_raw%d%d%d" % (side, n, b))
-                 for side in (Q, K) for n in range(IMAGES) for b in range(0, BLOCKS, h_step(side, n))}
-        w_raw = {(side, g, m): keep.tile([P, PACK, w_step(side, g)], BF16, name="w_raw%d%d%d" % (side, g, m))
-                 for side in (Q, K) for g in range(PASSES) for m in range(0, K_PASS, w_step(side, g))}
+                 for side in (Q, K) for n in range(IMAGES) for b in range(0, SLABS, h_step(side, n))}
+        w_raw = {(side, g, col): keep.tile([P, PACK, w_step(side, g)], BF16,
+                                           name="w_raw%d%d%d" % (side, g, col))
+                 for side in (Q, K) for g in range(PASSES) for col in range(0, K_PASS, w_step(side, g))}
         h_codes = [[keep.tile([P, C], U32, name="h_codes%d%d" % (side, n), align_bytes=64)
                     for n in range(IMAGES)] for side in (Q, K)]
         h_scales = [[keep.tile([P, C], U8, name="h_scales%d%d" % (side, n), align_bytes=64)
@@ -75,65 +76,65 @@ def tile_complexchannelattn_pa_kernel(tc, hq, hk, wq2, wk2, out):
                     for n in range(IMAGES)] for side in (Q, K)]
         a_scales = [[keep.tile([P, PASSES, C], U8, name="a_scales%d%d" % (side, n), align_bytes=64)
                      for n in range(IMAGES)] for side in (Q, K)]
-        s_parked = [keep.tile([P, C], F32, name="s_parked%d" % m) for m in range(BLOCKS)]
-        weights = [[keep.tile([P, C], F32, name="weights%d%d" % (n, m)) for m in range(BLOCKS)]
-                   for n in range(IMAGES)]
+        s_parked = [keep.tile([P, C], F32, name="s_parked%d" % m) for m in range(SLABS)]
+        probs = [[keep.tile([P, C], F32, name="probs%d%d" % (n, m)) for m in range(SLABS)]
+                 for n in range(IMAGES)]
 
-        def column(name):
-            return [[keep.tile([P, 1], F32, name="%s%d%d" % (name, n, m)) for m in range(BLOCKS)]
+        def per_row(name):
+            return [[keep.tile([P, 1], F32, name="%s%d%d" % (name, n, m)) for m in range(SLABS)]
                     for n in range(IMAGES)]
 
-        row_max, bias, row_sum, scale = column("row_max"), column("bias"), column("row_sum"), column("scale")
+        row_max, offset, row_sum, inv_sum = per_row("row_max"), per_row("offset"), per_row("row_sum"), per_row("inv_sum")
         ident = keep.tile([P, P], F32, name="ident")
         warm_in = keep.tile([P, 1], F32, name="warm_in")
         warm_out = keep.tile([P, 1], F32, name="warm_out")
 
         def load_h(side, n, b):
-            blocks = h_step(side, n)
+            slabs = h_step(side, n)
             nc.sync.dma_start(
-                out=h_raw[(side, n, b)][:].rearrange("p (b r) -> p b r", b=blocks),
-                in_=h_dram[side][n, P * b:P * (b + blocks), :].rearrange("(b p) r -> p b r", p=P))
+                out=h_raw[(side, n, b)][:].rearrange("p (b r) -> p b r", b=slabs),
+                in_=h_dram[side][n, P * b:P * (b + slabs), :].rearrange("(b p) r -> p b r", p=P))
 
-        def load_w(side, g, m):
-            lo = K_PASS * g + m
-            for u in range(2):
+        def load_w(side, g, col):
+            lo = K_PASS * g + col
+            for a in range(2):
                 nc.sync.dma_start(
-                    out=w_raw[(side, g, m)][:, 2 * u:2 * u + 2, :],
-                    in_=w_dram[side][2 * P * u:2 * P * (u + 1), lo:lo + w_step(side, g)].rearrange(
+                    out=w_raw[(side, g, col)][:, 2 * a:2 * a + 2, :],
+                    in_=w_dram[side][2 * P * a:2 * P * (a + 1), lo:lo + w_step(side, g)].rearrange(
                         "(p e) c -> p e c", e=2))
 
         load_h(Q, 0, 0)
-        for m in range(0, K_PASS, half):
-            load_w(Q, 0, m)
-        for b in range(1, BLOCKS):
+        for col in range(0, K_PASS, HALF_CHUNK):
+            load_w(Q, 0, col)
+        for b in range(1, SLABS):
             load_h(Q, 0, b)
-        for kind, side, i in operands[2:]:
+        for kind, side, which in operands[2:]:
             if kind == "h":
-                for b in range(0, BLOCKS, h_step(side, i)):
-                    load_h(side, i, b)
+                for b in range(0, SLABS, h_step(side, which)):
+                    load_h(side, which, b)
             else:
-                for m in range(0, K_PASS, w_step(side, i)):
-                    load_w(side, i, m)
+                for col in range(0, K_PASS, w_step(side, which)):
+                    load_w(side, which, col)
 
         make_identity(nc, ident[:])
         nc.vector.memset(warm_in[:], 0.0)
         nc.scalar.activation(out=warm_out[:], in_=warm_in[:], func=SIGMOID)
 
         def h_transposes(side, n, b0):
-            blocks = h_step(side, n)
-            planes = s_banks.tile([P, blocks, 2, P], F32, tag="s_banks", name="planes")
+            slabs = h_step(side, n)
+            planes = s_banks.tile([P, slabs, 2, P], F32, tag="s_banks", name="planes")
             words = h_raw[(side, n, b0)][:].bitcast(F32)
-            for b in range(blocks):
-                for u in range(2):
-                    lo = 2 * P * b + P * u
-                    nc.tensor.transpose(planes[:, b, u, :], words[:, lo:lo + P], ident[:])
+            for b in range(slabs):
+                for a in range(2):
+                    lo = 2 * P * b + P * a
+                    nc.tensor.transpose(planes[:, b, a, :], words[:, lo:lo + P], ident[:])
             return planes
 
         def h_copy(copy, side, n, planes, grouped, b0):
-            blocks = h_step(side, n)
-            dst = grouped[:].bitcast(F32)[:, 2 * P * b0:2 * P * (b0 + blocks)]
-            copy(out=dst.rearrange("p (b c u) -> p b c u", b=blocks, u=2),
-                 in_=planes[:].rearrange("p b u c -> p b c u"))
+            slabs = h_step(side, n)
+            dst = grouped[:].bitcast(F32)[:, 2 * P * b0:2 * P * (b0 + slabs)]
+            copy(out=dst.rearrange("p (b c a) -> p b c a", b=slabs, a=2),
+                 in_=planes[:].rearrange("p b a c -> p b c a"))
 
         def h_quantise(side, n, grouped, b0):
             c0, c1 = P * b0, P * (b0 + h_step(side, n))
@@ -141,45 +142,46 @@ def tile_complexchannelattn_pa_kernel(tc, hq, hk, wq2, wk2, out):
                                   scales=h_scales[side][n][:, c0:c1],
                                   in_=grouped[:, PACK * c0:PACK * c1])
 
-        def w_regroup(copy, side, g, grouped, m0, m1):
-            base = m0 - m0 % w_step(side, g)
-            copy(out=grouped[:, m0:m1, :].rearrange("p (c i) t -> p c t i", i=4),
-                 in_=w_raw[(side, g, base)][:, :, m0 - base:m1 - base].rearrange("p t (c i) -> p c t i", i=4))
+        def w_regroup(copy, side, g, grouped, col0, col1):
+            base = col0 - col0 % w_step(side, g)
+            copy(out=grouped[:, col0:col1, :].rearrange("p (c i) t -> p c t i", i=4),
+                 in_=w_raw[(side, g, base)][:, :, col0 - base:col1 - base].rearrange(
+                     "p t (c i) -> p c t i", i=4))
 
-        def w_quantise(side, g, grouped, m0, m1):
-            cols = slice(K_PASS * g + m0, K_PASS * g + m1)
-            nc.vector.quantize_mx(out=w_codes[side][:, cols].bitcast(FP8X4),
-                                  scales=w_scales[side][:, cols],
-                                  in_=grouped[:, m0:m1, :].rearrange("p m t -> p (m t)"))
+        def w_quantise(side, g, grouped, col0, col1):
+            lo = K_PASS * g
+            nc.vector.quantize_mx(out=w_codes[side][:, lo + col0:lo + col1].bitcast(FP8X4),
+                                  scales=w_scales[side][:, lo + col0:lo + col1],
+                                  in_=grouped[:, col0:col1, :].rearrange("p c t -> p (c t)"))
 
-        def prepare(kind, side, i):
+        def prepare(kind, side, which):
             if kind == "h":
-                starts = range(0, BLOCKS, h_step(side, i))
-                planes = [h_transposes(side, i, b) for b in starts]
+                starts = range(0, SLABS, h_step(side, which))
+                planes = [h_transposes(side, which, b) for b in starts]
                 grouped = h_stage.tile([P, PACK * C], BF16, name="h_grouped", align_bytes=64)
                 for b in starts:
-                    h_copy(nc.vector.tensor_copy, side, i, planes[b // 2], grouped, b)
+                    h_copy(nc.vector.tensor_copy, side, which, planes[b // 2], grouped, b)
                 for b in starts:
-                    h_quantise(side, i, grouped, b)
+                    h_quantise(side, which, grouped, b)
             else:
                 grouped = w_stage.tile([P, K_PASS, PACK], BF16, name="w_grouped", align_bytes=64)
-                for m in (0, half):
-                    w_regroup(nc.vector.tensor_copy, side, i, grouped, m, m + half)
-                for m in (0, half):
-                    w_quantise(side, i, grouped, m, m + half)
+                for col in (0, HALF_CHUNK):
+                    w_regroup(nc.vector.tensor_copy, side, which, grouped, col, col + HALF_CHUNK)
+                for col in (0, HALF_CHUNK):
+                    w_quantise(side, which, grouped, col, col + HALF_CHUNK)
 
         squashed = {}
 
-        def a_quantise(u, c0, c1):
-            side, n, g = unit_of(u)
+        def a_quantise(unit, c0, c1):
+            side, n, g = unit_of(unit)
             nc.vector.quantize_mx(out=a_codes[side][n][:, g, c0:c1].bitcast(FP8X4),
                                   scales=a_scales[side][n][:, g, c0:c1],
-                                  in_=squashed[u][:, PACK * c0:PACK * c1])
+                                  in_=squashed[unit][:, PACK * c0:PACK * c1])
 
-        def run_unit(u):
-            side, n, g = unit_of(u)
-            squashed[u] = a_stage.tile([P, PACK * C], BF16, name="squashed", align_bytes=64)
-            for b in range(BLOCKS):
+        def run_unit(unit):
+            side, n, g = unit_of(unit)
+            squashed[unit] = a_stage.tile([P, PACK * C], BF16, name="squashed", align_bytes=64)
+            for b in range(SLABS):
                 z = z_banks.tile([P, PACK, P], F32, tag="z_banks", name="z")
                 channels = slice(P * b, P * (b + 1))
                 for j in range(PACK):
@@ -191,15 +193,15 @@ def tile_complexchannelattn_pa_kernel(tc, hq, hk, wq2, wk2, out):
                                         rhs_scale=h_scales[side][n][:, channels],
                                         start=True, stop=True)
                 nc.scalar.activation(
-                    out=squashed[u][:, PACK * P * b:PACK * P * (b + 1)].rearrange("p (c j) -> p c j", j=PACK),
+                    out=squashed[unit][:, PACK * P * b:PACK * P * (b + 1)].rearrange("p (c j) -> p c j", j=PACK),
                     in_=z[:].rearrange("p j c -> p c j"), func=SIGMOID)
-                if u == UNITS - 1:
-                    a_quantise(u, P * b, P * (b + 1))
+                if unit == UNITS - 1:
+                    a_quantise(unit, P * b, P * (b + 1))
 
         s_open = {}
 
         def scores(n, g):
-            for m in range(BLOCKS):
+            for m in range(SLABS):
                 if g == 0:
                     s_open[(n, m)] = s_banks.tile([P, C], F32, tag="s_banks", name="s")
                 rows = slice(P * m, P * (m + 1))
@@ -213,68 +215,67 @@ def tile_complexchannelattn_pa_kernel(tc, hq, hk, wq2, wk2, out):
         def park(m):
             nc.vector.tensor_scalar(out=s_parked[m][:], in0=s_open[(0, m)][:], scalar1=inv, scalar2=None,
                                     op0=ALU.mult, op1=ALU.max, accum_out=row_max[0][m][:])
-            nc.vector.tensor_scalar(out=bias[0][m][:], in0=row_max[0][m][:], scalar1=-1.0, scalar2=-SHIFT,
+            nc.vector.tensor_scalar(out=offset[0][m][:], in0=row_max[0][m][:], scalar1=-1.0, scalar2=-SHIFT,
                                     op0=ALU.mult, op1=ALU.add)
 
         def maximum(m):
             nc.vector.tensor_reduce(out=row_max[1][m][:], in_=s_open[(1, m)][:],
                                     axis=mybir.AxisListType.X, op=ALU.max)
-            nc.vector.tensor_scalar(out=bias[1][m][:], in0=row_max[1][m][:], scalar1=-inv, scalar2=-SHIFT,
+            nc.vector.tensor_scalar(out=offset[1][m][:], in0=row_max[1][m][:], scalar1=-inv, scalar2=-SHIFT,
                                     op0=ALU.mult, op1=ALU.add)
 
         def exponentials(n, m):
-            nc.scalar.activation(out=weights[n][m][:], in_=(s_parked[m] if n == 0 else s_open[(n, m)])[:],
-                                 func=SIGMOID, bias=bias[n][m][:], scale=(1.0 if n == 0 else inv),
+            nc.scalar.activation(out=probs[n][m][:], in_=(s_parked[m] if n == 0 else s_open[(n, m)])[:],
+                                 func=SIGMOID, bias=offset[n][m][:], scale=(1.0 if n == 0 else inv),
                                  accum_out=row_sum[n][m][:])
 
         def normalise(engine, n, m):
-            nc.vector.reciprocal(out=scale[n][m][:], in_=row_sum[n][m][:])
-            engine.tensor_scalar(out=weights[n][m][:], in0=weights[n][m][:], scalar1=scale[n][m][:],
+            nc.vector.reciprocal(out=inv_sum[n][m][:], in_=row_sum[n][m][:])
+            engine.tensor_scalar(out=probs[n][m][:], in0=probs[n][m][:], scalar1=inv_sum[n][m][:],
                                  scalar2=0.0, op0=ALU.mult, op1=ALU.add)
-            nc.sync.dma_start(out=out[n, P * m:P * (m + 1), :], in_=weights[n][m][:])
+            nc.sync.dma_start(out=out[n, P * m:P * (m + 1), :], in_=probs[n][m][:])
 
         h_grouped0 = h_stage.tile([P, PACK * C], BF16, name="h_grouped", align_bytes=64)
         w_grouped0 = w_stage.tile([P, K_PASS, PACK], BF16, name="w_grouped", align_bytes=64)
 
-        def first_block(b, copy):
+        def first_slab(b):
             planes = h_transposes(Q, 0, b)
-            h_copy(copy, Q, 0, planes, h_grouped0, b)
+            h_copy(nc.scalar.copy, Q, 0, planes, h_grouped0, b)
             h_quantise(Q, 0, h_grouped0, b)
 
-        first_block(0, nc.scalar.copy)
-        w_regroup(nc.vector.tensor_copy, Q, 0, w_grouped0, 0, half)
-        w_quantise(Q, 0, w_grouped0, 0, half)
-        w_regroup(nc.vector.tensor_copy, Q, 0, w_grouped0, half, half + P)
-        w_regroup(nc.scalar.copy, Q, 0, w_grouped0, half + P, K_PASS)
-        w_quantise(Q, 0, w_grouped0, half, K_PASS)
-        for b in range(1, BLOCKS):
-            first_block(b, nc.scalar.copy if b < BLOCKS - 1 else nc.vector.tensor_copy)
+        first_slab(0)
+        w_regroup(nc.vector.tensor_copy, Q, 0, w_grouped0, 0, HALF_CHUNK)
+        w_quantise(Q, 0, w_grouped0, 0, HALF_CHUNK)
+        w_regroup(nc.vector.tensor_copy, Q, 0, w_grouped0, HALF_CHUNK, HALF_CHUNK + P)
+        w_regroup(nc.scalar.copy, Q, 0, w_grouped0, HALF_CHUNK + P, K_PASS)
+        w_quantise(Q, 0, w_grouped0, HALF_CHUNK, K_PASS)
+        for b in range(1, SLABS):
+            first_slab(b)
 
-        for u in range(UNITS):
-            side, n, g = unit_of(u)
-            if u + 2 < len(operands):
-                prepare(*operands[u + 2])
-            run_unit(u)
-            if u >= SCORE_LAG and unit_of(u - SCORE_LAG)[:2] == (K, 0):
-                scores(0, unit_of(u - SCORE_LAG)[2])
-                if unit_of(u - SCORE_LAG)[2] == PASSES - 1:
-                    for m in range(BLOCKS):
+        for unit in range(UNITS):
+            if unit + 2 < len(operands):
+                prepare(*operands[unit + 2])
+            run_unit(unit)
+            if unit >= SCORE_LAG and unit_of(unit - SCORE_LAG)[:2] == (K, 0):
+                scores(0, unit_of(unit - SCORE_LAG)[2])
+                if unit_of(unit - SCORE_LAG)[2] == PASSES - 1:
+                    for m in range(SLABS):
                         park(m)
-            if PASSES <= u < PASSES + IMAGES * PASSES:
-                a_quantise(u - PASSES, 0, C)
-            if side == K and u < UNITS - 1:
-                a_quantise(u, 0, C)
+            if PASSES <= unit < PASSES + IMAGES * PASSES:
+                a_quantise(unit - PASSES, 0, C)
+            if unit_of(unit)[0] == K and unit < UNITS - 1:
+                a_quantise(unit, 0, C)
 
         for g in range(PASSES):
             scores(1, g)
-        for m in range(BLOCKS):
+        for m in range(SLABS):
             exponentials(0, m)
-        for m in range(BLOCKS // 2):
+        for m in range(SLABS // 2):
             normalise(nc.vector, 0, m)
-        for m in range(BLOCKS):
-            if m < BLOCKS // 2:
-                normalise(nc.gpsimd, 0, m + BLOCKS // 2)
+        for m in range(SLABS):
+            if m < SLABS // 2:
+                normalise(nc.gpsimd, 0, m + SLABS // 2)
             maximum(m)
-        for m in range(BLOCKS):
+        for m in range(SLABS):
             exponentials(1, m)
             normalise(nc.vector, 1, m)

@@ -170,6 +170,42 @@ def tile_complexchannelattn_pa_kernel(tc, hq, hk, wq2, wk2, out):
                 for col in (0, HALF_CHUNK):
                     w_quantise(side, which, grouped, col, col + HALF_CHUNK)
 
+        s_open = {}
+
+        def score_pass(n, g, m):
+            if g == 0:
+                s_open[(n, m)] = s_banks.tile([P, C], F32, tag="s_banks", name="s")
+            rows = slice(P * m, P * (m + 1))
+            nc.tensor.matmul_mx(out=s_open[(n, m)][:],
+                                lhsT=a_codes[Q][n][:, g, rows].bitcast(FP8X4),
+                                lhsT_scale=a_scales[Q][n][:, g, rows],
+                                rhs=a_codes[K][n][:, g, :].bitcast(FP8X4),
+                                rhs_scale=a_scales[K][n][:, g, :],
+                                start=(g == 0), stop=(g == PASSES - 1))
+
+        def park(m):
+            nc.vector.tensor_scalar(out=s_parked[m][:], in0=s_open[(0, m)][:], scalar1=inv, scalar2=None,
+                                    op0=ALU.mult, op1=ALU.max, accum_out=row_max[0][m][:])
+            nc.vector.tensor_scalar(out=offset[0][m][:], in0=row_max[0][m][:], scalar1=-1.0, scalar2=-SHIFT,
+                                    op0=ALU.mult, op1=ALU.add)
+
+        def maximum(m):
+            nc.vector.tensor_reduce(out=row_max[1][m][:], in_=s_open[(1, m)][:],
+                                    axis=mybir.AxisListType.X, op=ALU.max)
+            nc.vector.tensor_scalar(out=offset[1][m][:], in0=row_max[1][m][:], scalar1=-inv, scalar2=-SHIFT,
+                                    op0=ALU.mult, op1=ALU.add)
+
+        def exponentials(n, m):
+            nc.scalar.activation(out=probs[n][m][:], in_=(s_parked[m] if n == 0 else s_open[(n, m)])[:],
+                                 func=SIGMOID, bias=offset[n][m][:], scale=(1.0 if n == 0 else inv),
+                                 accum_out=row_sum[n][m][:])
+
+        def normalise(engine, n, m):
+            nc.vector.reciprocal(out=inv_sum[n][m][:], in_=row_sum[n][m][:])
+            engine.tensor_scalar(out=probs[n][m][:], in0=probs[n][m][:], scalar1=inv_sum[n][m][:],
+                                 scalar2=0.0, op0=ALU.mult, op1=ALU.add)
+            nc.sync.dma_start(out=out[n, P * m:P * (m + 1), :], in_=probs[n][m][:])
+
         squashed = {}
 
         def a_quantise(unit, c0, c1):
@@ -195,45 +231,14 @@ def tile_complexchannelattn_pa_kernel(tc, hq, hk, wq2, wk2, out):
                 nc.scalar.activation(
                     out=squashed[unit][:, PACK * P * b:PACK * P * (b + 1)].rearrange("p (c j) -> p c j", j=PACK),
                     in_=z[:].rearrange("p j c -> p c j"), func=SIGMOID)
+                if unit >= SCORE_LAG and unit_of(unit - SCORE_LAG)[0] == K:
+                    score_pass(*unit_of(unit - SCORE_LAG)[1:], b)
+                    if unit_of(unit - SCORE_LAG)[1:] == (0, PASSES - 1):
+                        park(b)
+                if b == 0 and unit_of(unit - 1)[0] == K:
+                    a_quantise(unit - 1, 0, C)
                 if unit == UNITS - 1:
                     a_quantise(unit, P * b, P * (b + 1))
-
-        s_open = {}
-
-        def scores(n, g):
-            for m in range(SLABS):
-                if g == 0:
-                    s_open[(n, m)] = s_banks.tile([P, C], F32, tag="s_banks", name="s")
-                rows = slice(P * m, P * (m + 1))
-                nc.tensor.matmul_mx(out=s_open[(n, m)][:],
-                                    lhsT=a_codes[Q][n][:, g, rows].bitcast(FP8X4),
-                                    lhsT_scale=a_scales[Q][n][:, g, rows],
-                                    rhs=a_codes[K][n][:, g, :].bitcast(FP8X4),
-                                    rhs_scale=a_scales[K][n][:, g, :],
-                                    start=(g == 0), stop=(g == PASSES - 1))
-
-        def park(m):
-            nc.vector.tensor_scalar(out=s_parked[m][:], in0=s_open[(0, m)][:], scalar1=inv, scalar2=None,
-                                    op0=ALU.mult, op1=ALU.max, accum_out=row_max[0][m][:])
-            nc.vector.tensor_scalar(out=offset[0][m][:], in0=row_max[0][m][:], scalar1=-1.0, scalar2=-SHIFT,
-                                    op0=ALU.mult, op1=ALU.add)
-
-        def maximum(m):
-            nc.vector.tensor_reduce(out=row_max[1][m][:], in_=s_open[(1, m)][:],
-                                    axis=mybir.AxisListType.X, op=ALU.max)
-            nc.vector.tensor_scalar(out=offset[1][m][:], in0=row_max[1][m][:], scalar1=-inv, scalar2=-SHIFT,
-                                    op0=ALU.mult, op1=ALU.add)
-
-        def exponentials(n, m):
-            nc.scalar.activation(out=probs[n][m][:], in_=(s_parked[m] if n == 0 else s_open[(n, m)])[:],
-                                 func=SIGMOID, bias=offset[n][m][:], scale=(1.0 if n == 0 else inv),
-                                 accum_out=row_sum[n][m][:])
-
-        def normalise(engine, n, m):
-            nc.vector.reciprocal(out=inv_sum[n][m][:], in_=row_sum[n][m][:])
-            engine.tensor_scalar(out=probs[n][m][:], in0=probs[n][m][:], scalar1=inv_sum[n][m][:],
-                                 scalar2=0.0, op0=ALU.mult, op1=ALU.add)
-            nc.sync.dma_start(out=out[n, P * m:P * (m + 1), :], in_=probs[n][m][:])
 
         h_grouped0 = h_stage.tile([P, PACK * C], BF16, name="h_grouped", align_bytes=64)
         w_grouped0 = w_stage.tile([P, K_PASS, PACK], BF16, name="w_grouped", align_bytes=64)
@@ -255,27 +260,23 @@ def tile_complexchannelattn_pa_kernel(tc, hq, hk, wq2, wk2, out):
         for unit in range(UNITS):
             if unit + 2 < len(operands):
                 prepare(*operands[unit + 2])
-            run_unit(unit)
-            if unit >= SCORE_LAG and unit_of(unit - SCORE_LAG)[:2] == (K, 0):
-                scores(0, unit_of(unit - SCORE_LAG)[2])
-                if unit_of(unit - SCORE_LAG)[2] == PASSES - 1:
-                    for m in range(SLABS):
-                        park(m)
             if PASSES <= unit < PASSES + IMAGES * PASSES:
                 a_quantise(unit - PASSES, 0, C)
-            if unit_of(unit)[0] == K and unit < UNITS - 1:
-                a_quantise(unit, 0, C)
+            if unit == UNITS - 2:
+                exponentials(0, 0)
+            if unit == UNITS - 1:
+                normalise(nc.vector, 0, 0)
+            run_unit(unit)
 
-        for g in range(PASSES):
-            scores(1, g)
-        for m in range(SLABS):
+        for unit in range(UNITS - SCORE_LAG, UNITS):
+            for m in range(SLABS):
+                score_pass(*unit_of(unit)[1:], m)
+        for m in range(1, SLABS):
             exponentials(0, m)
-        for m in range(SLABS // 2):
-            normalise(nc.vector, 0, m)
         for m in range(SLABS):
-            if m < SLABS // 2:
-                normalise(nc.gpsimd, 0, m + SLABS // 2)
             maximum(m)
+            if m > 0:
+                normalise(nc.gpsimd, 0, m)
         for m in range(SLABS):
             exponentials(1, m)
             normalise(nc.vector, 1, m)

@@ -25,6 +25,8 @@ SLABS = C // P
 Q = 0
 K = 1
 UNITS = 2 * IMAGES * PASSES
+TRB = 1
+Q_LAG = (6, 6)
 SCORE_LAG = 2
 SHIFT = 24.0
 FLOPS = 2 * 2 * IMAGES * C * R * HW + 2 * IMAGES * C * C * HW
@@ -37,7 +39,9 @@ def tile_complexchannelattn_pa_kernel(tc, hq, hk, wq2, wk2, out):
     inv = 1.0 / math.sqrt(C)
 
     def unit_of(unit):
-        return unit // (IMAGES * PASSES), (unit // PASSES) % IMAGES, unit % PASSES
+        side, u = divmod(unit, IMAGES * PASSES)
+        n, g = (u % IMAGES, u // IMAGES) if side == Q else (u // PASSES, u % PASSES)
+        return side, n, g
 
     operands = []
     for unit in range(UNITS):
@@ -47,7 +51,7 @@ def tile_complexchannelattn_pa_kernel(tc, hq, hk, wq2, wk2, out):
                 operands.append(operand)
 
     def h_step(side, n):
-        return 1 if (side, n) == (Q, 0) else 2
+        return 1 if side == Q else 2
 
     def w_step(side, g):
         return HALF_CHUNK if side == Q and g < 2 else K_PASS
@@ -56,7 +60,7 @@ def tile_complexchannelattn_pa_kernel(tc, hq, hk, wq2, wk2, out):
         keep = ctx.enter_context(tc.tile_pool(name="keep", bufs=1))
         w_stage = ctx.enter_context(tc.tile_pool(name="w_stage", bufs=2))
         h_stage = ctx.enter_context(tc.tile_pool(name="h_stage", bufs=2))
-        a_stage = ctx.enter_context(tc.tile_pool(name="a_stage", bufs=2 * PASSES))
+        a_stage = ctx.enter_context(tc.tile_pool(name="a_stage", bufs=12))
         z_banks = ctx.enter_context(tc.psum_pool(name="z_banks", bufs=4))
         s_banks = ctx.enter_context(tc.psum_pool(name="s_banks", bufs=4))
         ctx.enter_context(tc.manual_schedule())
@@ -154,15 +158,23 @@ def tile_complexchannelattn_pa_kernel(tc, hq, hk, wq2, wk2, out):
                                   scales=w_scales[side][:, lo + col0:lo + col1],
                                   in_=grouped[:, col0:col1, :].rearrange("p c t -> p (c t)"))
 
+        early = {}
+
+        def transposes(kind, side, which):
+            if kind == "h":
+                early[(side, which)] = [h_transposes(side, which, b) for b in range(0, SLABS, h_step(side, which))]
+
         def prepare(kind, side, which):
             if kind == "h":
                 starts = range(0, SLABS, h_step(side, which))
-                planes = [h_transposes(side, which, b) for b in starts]
+                planes = early.pop((side, which))
                 grouped = h_stage.tile([P, PACK * C], BF16, name="h_grouped", align_bytes=64)
+                step = h_step(side, which)
                 for b in starts:
-                    h_copy(nc.vector.tensor_copy, side, which, planes[b // 2], grouped, b)
-                for b in starts:
-                    h_quantise(side, which, grouped, b)
+                    h_copy(nc.vector.tensor_copy, side, which, planes[b // step], grouped, b)
+                    if b > 0:
+                        h_quantise(side, which, grouped, b - step)
+                h_quantise(side, which, grouped, SLABS - step)
             else:
                 grouped = w_stage.tile([P, K_PASS, PACK], BF16, name="w_grouped", align_bytes=64)
                 for col in (0, HALF_CHUNK):
@@ -192,6 +204,8 @@ def tile_complexchannelattn_pa_kernel(tc, hq, hk, wq2, wk2, out):
         def maximum(m):
             nc.vector.tensor_reduce(out=row_max[1][m][:], in_=s_open[(1, m)][:],
                                     axis=mybir.AxisListType.X, op=ALU.max)
+
+        def shift(m):
             nc.vector.tensor_scalar(out=offset[1][m][:], in0=row_max[1][m][:], scalar1=-inv, scalar2=-SHIFT,
                                     op0=ALU.mult, op1=ALU.add)
 
@@ -200,8 +214,10 @@ def tile_complexchannelattn_pa_kernel(tc, hq, hk, wq2, wk2, out):
                                  func=SIGMOID, bias=offset[n][m][:], scale=(1.0 if n == 0 else inv),
                                  accum_out=row_sum[n][m][:])
 
-        def normalise(engine, n, m):
+        def invert(n, m):
             nc.vector.reciprocal(out=inv_sum[n][m][:], in_=row_sum[n][m][:])
+
+        def normalise(engine, n, m):
             engine.tensor_scalar(out=probs[n][m][:], in0=probs[n][m][:], scalar1=inv_sum[n][m][:],
                                  scalar2=0.0, op0=ALU.mult, op1=ALU.add)
             nc.sync.dma_start(out=out[n, P * m:P * (m + 1), :], in_=probs[n][m][:])
@@ -231,6 +247,8 @@ def tile_complexchannelattn_pa_kernel(tc, hq, hk, wq2, wk2, out):
                 nc.scalar.activation(
                     out=squashed[unit][:, PACK * P * b:PACK * P * (b + 1)].rearrange("p (c j) -> p c j", j=PACK),
                     in_=z[:].rearrange("p j c -> p c j"), func=SIGMOID)
+                if unit == 0 and b == TRB:
+                    transposes(*prep[0])
                 if unit >= SCORE_LAG and unit_of(unit - SCORE_LAG)[0] == K:
                     score_pass(*unit_of(unit - SCORE_LAG)[1:], b)
                     if unit_of(unit - SCORE_LAG)[1:] == (0, PASSES - 1):
@@ -248,35 +266,49 @@ def tile_complexchannelattn_pa_kernel(tc, hq, hk, wq2, wk2, out):
             h_copy(nc.scalar.copy, Q, 0, planes, h_grouped0, b)
             h_quantise(Q, 0, h_grouped0, b)
 
-        first_slab(0)
         w_regroup(nc.vector.tensor_copy, Q, 0, w_grouped0, 0, HALF_CHUNK)
-        w_quantise(Q, 0, w_grouped0, 0, HALF_CHUNK)
+        first_slab(0)
         w_regroup(nc.vector.tensor_copy, Q, 0, w_grouped0, HALF_CHUNK, HALF_CHUNK + P)
         w_regroup(nc.scalar.copy, Q, 0, w_grouped0, HALF_CHUNK + P, K_PASS)
+        w_quantise(Q, 0, w_grouped0, 0, HALF_CHUNK)
         w_quantise(Q, 0, w_grouped0, HALF_CHUNK, K_PASS)
         for b in range(1, SLABS):
             first_slab(b)
 
+        prep = operands[2:9] + [operands[11]] + operands[9:11]
         for unit in range(UNITS):
-            if unit + 2 < len(operands):
-                prepare(*operands[unit + 2])
-            if PASSES <= unit < PASSES + IMAGES * PASSES:
-                a_quantise(unit - PASSES, 0, C)
+            for n in range(IMAGES):
+                q = unit - Q_LAG[n]
+                if q >= 0 and unit_of(q)[:2] == (Q, n):
+                    a_quantise(q, 0, C)
             if unit == UNITS - 2:
                 exponentials(0, 0)
             if unit == UNITS - 1:
+                invert(0, 0)
                 normalise(nc.vector, 0, 0)
             run_unit(unit)
+            if unit < len(prep):
+                prepare(*prep[unit])
+            if unit + 1 < len(prep):
+                transposes(*prep[unit + 1])
 
         for unit in range(UNITS - SCORE_LAG, UNITS):
             for m in range(SLABS):
                 score_pass(*unit_of(unit)[1:], m)
         for m in range(1, SLABS):
             exponentials(0, m)
+        invert(0, 1)
+        normalise(nc.gpsimd, 0, 1)
         for m in range(SLABS):
             maximum(m)
-            if m > 0:
-                normalise(nc.gpsimd, 0, m)
-        for m in range(SLABS):
+            if m < 2:
+                invert(0, m + 2)
+                normalise(nc.gpsimd, 0, m + 2)
+            if m == 2:
+                invert(1, 0)
+                normalise(nc.gpsimd, 1, 0)
+            shift(m)
             exponentials(1, m)
+        for m in range(1, SLABS):
+            invert(1, m)
             normalise(nc.vector, 1, m)

@@ -22,8 +22,8 @@ HW = 2048
 PASSES = HW // K_PASS
 HALF_CHUNK = K_PASS // 2
 SLABS = C // P
-Q = 0
-K = 1
+K = 0
+Q = 1
 UNITS = 2 * IMAGES * PASSES
 TRB = 1
 Q_LAG = (6, 6)
@@ -34,14 +34,14 @@ FLOPS = 2 * 2 * IMAGES * C * R * HW + 2 * IMAGES * C * C * HW
 
 def tile_complexchannelattn_pa_kernel(tc, hq, hk, wq2, wk2, out):
     nc = tc.nc
-    h_dram = (hq, hk)
-    w_dram = (wq2, wk2)
+    h_dram = (hk, hq)
+    w_dram = (wk2, wq2)
     inv = 1.0 / math.sqrt(C)
 
     def unit_of(unit):
         side, u = divmod(unit, IMAGES * PASSES)
-        n, g = (u % IMAGES, u // IMAGES) if side == Q else (u // PASSES, u % PASSES)
-        return side, n, g
+        n, part = (u % IMAGES, u // IMAGES) if side == K else (u // PASSES, u % PASSES)
+        return side, n, part
 
     operands = []
     for unit in range(UNITS):
@@ -51,10 +51,10 @@ def tile_complexchannelattn_pa_kernel(tc, hq, hk, wq2, wk2, out):
                 operands.append(operand)
 
     def h_step(side, n):
-        return 1 if side == Q else 2
+        return 1 if side == K else 2
 
     def w_step(side, g):
-        return HALF_CHUNK if side == Q and g < 2 else K_PASS
+        return HALF_CHUNK if side == K and g < 2 else K_PASS
 
     with ExitStack() as ctx:
         keep = ctx.enter_context(tc.tile_pool(name="keep", bufs=1))
@@ -66,20 +66,20 @@ def tile_complexchannelattn_pa_kernel(tc, hq, hk, wq2, wk2, out):
         ctx.enter_context(tc.manual_schedule())
 
         h_raw = {(side, n, b): keep.tile([P, h_step(side, n) * R], BF16, name="h_raw%d%d%d" % (side, n, b))
-                 for side in (Q, K) for n in range(IMAGES) for b in range(0, SLABS, h_step(side, n))}
+                 for side in (K, Q) for n in range(IMAGES) for b in range(0, SLABS, h_step(side, n))}
         w_raw = {(side, g, col): keep.tile([P, PACK, w_step(side, g)], BF16,
                                            name="w_raw%d%d%d" % (side, g, col))
-                 for side in (Q, K) for g in range(PASSES) for col in range(0, K_PASS, w_step(side, g))}
+                 for side in (K, Q) for g in range(PASSES) for col in range(0, K_PASS, w_step(side, g))}
         h_codes = [[keep.tile([P, C], U32, name="h_codes%d%d" % (side, n), align_bytes=64)
-                    for n in range(IMAGES)] for side in (Q, K)]
+                    for n in range(IMAGES)] for side in (K, Q)]
         h_scales = [[keep.tile([P, C], U8, name="h_scales%d%d" % (side, n), align_bytes=64)
-                     for n in range(IMAGES)] for side in (Q, K)]
-        w_codes = [keep.tile([P, HW], U32, name="w_codes%d" % side, align_bytes=64) for side in (Q, K)]
-        w_scales = [keep.tile([P, HW], U8, name="w_scales%d" % side, align_bytes=64) for side in (Q, K)]
+                     for n in range(IMAGES)] for side in (K, Q)]
+        w_codes = [keep.tile([P, HW], U32, name="w_codes%d" % side, align_bytes=64) for side in (K, Q)]
+        w_scales = [keep.tile([P, HW], U8, name="w_scales%d" % side, align_bytes=64) for side in (K, Q)]
         a_codes = [[keep.tile([P, PASSES, C], U32, name="a_codes%d%d" % (side, n), align_bytes=64)
-                    for n in range(IMAGES)] for side in (Q, K)]
+                    for n in range(IMAGES)] for side in (K, Q)]
         a_scales = [[keep.tile([P, PASSES, C], U8, name="a_scales%d%d" % (side, n), align_bytes=64)
-                     for n in range(IMAGES)] for side in (Q, K)]
+                     for n in range(IMAGES)] for side in (K, Q)]
         s_parked = [keep.tile([P, C], F32, name="s_parked%d" % m) for m in range(SLABS)]
         probs = [[keep.tile([P, C], F32, name="probs%d%d" % (n, m)) for m in range(SLABS)]
                  for n in range(IMAGES)]
@@ -107,11 +107,11 @@ def tile_complexchannelattn_pa_kernel(tc, hq, hk, wq2, wk2, out):
                     in_=w_dram[side][2 * P * a:2 * P * (a + 1), lo:lo + w_step(side, g)].rearrange(
                         "(p e) c -> p e c", e=2))
 
-        load_h(Q, 0, 0)
+        load_h(K, 0, 0)
         for col in range(0, K_PASS, HALF_CHUNK):
-            load_w(Q, 0, col)
+            load_w(K, 0, col)
         for b in range(1, SLABS):
-            load_h(Q, 0, b)
+            load_h(K, 0, b)
         for kind, side, which in operands[2:]:
             if kind == "h":
                 for b in range(0, SLABS, h_step(side, which)):
@@ -187,10 +187,11 @@ def tile_complexchannelattn_pa_kernel(tc, hq, hk, wq2, wk2, out):
         def score_pass(n, g, m):
             if g == 0:
                 s_open[(n, m)] = s_banks.tile([P, C], F32, tag="s_banks", name="s")
-            rows = slice(P * m, P * (m + 1))
+            part, i = (m, g) if n == 1 else (g, m)
+            words = slice(P * i, P * (i + 1))
             nc.tensor.matmul_mx(out=s_open[(n, m)][:],
-                                lhsT=a_codes[Q][n][:, g, rows].bitcast(FP8X4),
-                                lhsT_scale=a_scales[Q][n][:, g, rows],
+                                lhsT=a_codes[Q][n][:, part, words].bitcast(FP8X4),
+                                lhsT_scale=a_scales[Q][n][:, part, words],
                                 rhs=a_codes[K][n][:, g, :].bitcast(FP8X4),
                                 rhs_scale=a_scales[K][n][:, g, :],
                                 start=(g == 0), stop=(g == PASSES - 1))
@@ -224,54 +225,72 @@ def tile_complexchannelattn_pa_kernel(tc, hq, hk, wq2, wk2, out):
 
         squashed = {}
 
-        def a_quantise(unit, c0, c1):
-            side, n, g = unit_of(unit)
-            nc.vector.quantize_mx(out=a_codes[side][n][:, g, c0:c1].bitcast(FP8X4),
-                                  scales=a_scales[side][n][:, g, c0:c1],
-                                  in_=squashed[unit][:, PACK * c0:PACK * c1])
+        def a_quantise(unit, i0, i1):
+            side, n, part = unit_of(unit)
+            nc.vector.quantize_mx(out=a_codes[side][n][:, part, P * i0:P * i1].bitcast(FP8X4),
+                                  scales=a_scales[side][n][:, part, P * i0:P * i1],
+                                  in_=squashed[unit][:, PACK * P * i0:PACK * P * i1])
+
+        def bank(unit, i):
+            side, n, part = unit_of(unit)
+            g, b = (i, part) if (side, n) == (Q, 1) else (part, i)
+            z = z_banks.tile([P, PACK, P], F32, tag="z_banks", name="z")
+            channels = slice(P * b, P * (b + 1))
+            for j in range(PACK):
+                positions = slice(K_PASS * g + P * j, K_PASS * g + P * (j + 1))
+                nc.tensor.matmul_mx(out=z[:, j, :],
+                                    lhsT=w_codes[side][:, positions].bitcast(FP8X4),
+                                    lhsT_scale=w_scales[side][:, positions],
+                                    rhs=h_codes[side][n][:, channels].bitcast(FP8X4),
+                                    rhs_scale=h_scales[side][n][:, channels],
+                                    start=True, stop=True)
+            nc.scalar.activation(
+                out=squashed[unit][:, PACK * P * i:PACK * P * (i + 1)].rearrange("p (c j) -> p c j", j=PACK),
+                in_=z[:].rearrange("p j c -> p c j"), func=SIGMOID)
+
+        TILES = [(n, m) for n in range(IMAGES) for m in range(SLABS)]
 
         def run_unit(unit):
-            side, n, g = unit_of(unit)
             squashed[unit] = a_stage.tile([P, PACK * C], BF16, name="squashed", align_bytes=64)
-            for b in range(SLABS):
-                z = z_banks.tile([P, PACK, P], F32, tag="z_banks", name="z")
-                channels = slice(P * b, P * (b + 1))
-                for j in range(PACK):
-                    positions = slice(K_PASS * g + P * j, K_PASS * g + P * (j + 1))
-                    nc.tensor.matmul_mx(out=z[:, j, :],
-                                        lhsT=w_codes[side][:, positions].bitcast(FP8X4),
-                                        lhsT_scale=w_scales[side][:, positions],
-                                        rhs=h_codes[side][n][:, channels].bitcast(FP8X4),
-                                        rhs_scale=h_scales[side][n][:, channels],
-                                        start=True, stop=True)
-                nc.scalar.activation(
-                    out=squashed[unit][:, PACK * P * b:PACK * P * (b + 1)].rearrange("p (c j) -> p c j", j=PACK),
-                    in_=z[:].rearrange("p j c -> p c j"), func=SIGMOID)
-                if unit == 0 and b == TRB:
+            for i in range(SLABS):
+                bank(unit, i)
+                if unit == 0 and i == 1:
                     transposes(*prep[0])
-                if unit >= SCORE_LAG and unit_of(unit - SCORE_LAG)[0] == K:
-                    score_pass(*unit_of(unit - SCORE_LAG)[1:], b)
-                    if unit_of(unit - SCORE_LAG)[1:] == (0, PASSES - 1):
-                        park(b)
-                if b == 0 and unit_of(unit - 1)[0] == K:
-                    a_quantise(unit - 1, 0, C)
-                if unit == UNITS - 1:
-                    a_quantise(unit, P * b, P * (b + 1))
+                if unit >= SCORE_LAG and unit_of(unit - SCORE_LAG)[0] == Q:
+                    n, part = unit_of(unit - SCORE_LAG)[1:]
+                    for x in range(2*i, min(2*i + 2, SLABS)) if n else (i,):
+                        score_pass(n, x if n else part, part if n else x)
+                        if (n, part) == (0, PASSES - 1):
+                            park(x)
+                if unit >= UNITS - 2 and i == 1:
+                    maximum(unit - UNITS + 2)
+                if i == 0 and unit_of(unit - 1)[0] == Q and unit - 1 < 15:
+                    a_quantise(unit - 1, 0, SLABS)
+                if unit >= 15:
+                    a_quantise(unit, i, i + 1)
+                if unit >= UNITS - 2 and i == 1:
+                    shift(unit - UNITS + 2)
+                step = 2 * (unit - (UNITS - 3)) + i // 2 - 1
+                if i % 2 == 1 and 0 <= step < 4:
+                    exponentials(*TILES[step])
+                if i % 2 == 0 and 0 < step <= 4:
+                    invert(*TILES[step - 1])
+                    normalise(nc.vector, *TILES[step - 1])
 
         h_grouped0 = h_stage.tile([P, PACK * C], BF16, name="h_grouped", align_bytes=64)
         w_grouped0 = w_stage.tile([P, K_PASS, PACK], BF16, name="w_grouped", align_bytes=64)
 
         def first_slab(b):
-            planes = h_transposes(Q, 0, b)
-            h_copy(nc.scalar.copy, Q, 0, planes, h_grouped0, b)
-            h_quantise(Q, 0, h_grouped0, b)
+            planes = h_transposes(K, 0, b)
+            h_copy(nc.scalar.copy, K, 0, planes, h_grouped0, b)
+            h_quantise(K, 0, h_grouped0, b)
 
-        w_regroup(nc.vector.tensor_copy, Q, 0, w_grouped0, 0, HALF_CHUNK)
+        w_regroup(nc.vector.tensor_copy, K, 0, w_grouped0, 0, HALF_CHUNK)
         first_slab(0)
-        w_regroup(nc.vector.tensor_copy, Q, 0, w_grouped0, HALF_CHUNK, HALF_CHUNK + P)
-        w_regroup(nc.scalar.copy, Q, 0, w_grouped0, HALF_CHUNK + P, K_PASS)
-        w_quantise(Q, 0, w_grouped0, 0, HALF_CHUNK)
-        w_quantise(Q, 0, w_grouped0, HALF_CHUNK, K_PASS)
+        w_regroup(nc.vector.tensor_copy, K, 0, w_grouped0, HALF_CHUNK, HALF_CHUNK + P)
+        w_regroup(nc.scalar.copy, K, 0, w_grouped0, HALF_CHUNK + P, K_PASS)
+        w_quantise(K, 0, w_grouped0, 0, HALF_CHUNK)
+        w_quantise(K, 0, w_grouped0, HALF_CHUNK, K_PASS)
         for b in range(1, SLABS):
             first_slab(b)
 
@@ -279,36 +298,31 @@ def tile_complexchannelattn_pa_kernel(tc, hq, hk, wq2, wk2, out):
         for unit in range(UNITS):
             for n in range(IMAGES):
                 q = unit - Q_LAG[n]
-                if q >= 0 and unit_of(q)[:2] == (Q, n):
-                    a_quantise(q, 0, C)
-            if unit == UNITS - 2:
-                exponentials(0, 0)
-            if unit == UNITS - 1:
-                invert(0, 0)
-                normalise(nc.vector, 0, 0)
+                if q >= 0 and unit_of(q)[:2] == (K, n):
+                    a_quantise(q, 0, SLABS)
             run_unit(unit)
             if unit < len(prep):
                 prepare(*prep[unit])
             if unit + 1 < len(prep):
                 transposes(*prep[unit + 1])
 
-        for unit in range(UNITS - SCORE_LAG, UNITS):
-            for m in range(SLABS):
-                score_pass(*unit_of(unit)[1:], m)
-        for m in range(1, SLABS):
-            exponentials(0, m)
-        invert(0, 1)
-        normalise(nc.gpsimd, 0, 1)
-        for m in range(SLABS):
-            maximum(m)
-            if m < 2:
-                invert(0, m + 2)
-                normalise(nc.gpsimd, 0, m + 2)
-            if m == 2:
-                invert(1, 0)
-                normalise(nc.gpsimd, 1, 0)
-            shift(m)
-            exponentials(1, m)
-        for m in range(1, SLABS):
-            invert(1, m)
-            normalise(nc.vector, 1, m)
+        exponentials(1, 0)
+        exponentials(1, 1)
+        for g in range(PASSES):
+            score_pass(1, g, 2)
+        maximum(2)
+        invert(1, 0)
+        shift(2)
+        exponentials(1, 2)
+        normalise(nc.vector, 1, 0)
+        for g in range(PASSES):
+            score_pass(1, g, 3)
+        maximum(3)
+        invert(1, 1)
+        shift(3)
+        exponentials(1, 3)
+        normalise(nc.vector, 1, 1)
+        invert(1, 2)
+        normalise(nc.vector, 1, 2)
+        invert(1, 3)
+        normalise(nc.vector, 1, 3)

@@ -121,6 +121,15 @@ def tile_complexchannelattn_pa_kernel(tc, hq, hk, wq2, wk2, out):
                     load_w(side, which, col)
 
         make_identity(nc, ident[:])
+        heat = keep.tile([P, C], BF16, name="heat")
+        nc.vector.memset(heat[:], 0.0)
+
+        def warm_up(count):
+            idle = z_banks.tile([P, PACK, P], F32, tag="z_banks", name="idle")
+            for turn in range(count):
+                nc.tensor.matmul(out=idle[:].rearrange("p j c -> p (j c)"), lhsT=heat[:, :P], rhs=heat[:],
+                                 start=True, stop=True)
+
         nc.vector.memset(warm_in[:], 0.0)
         nc.scalar.activation(out=warm_out[:], in_=warm_in[:], func=SIGMOID)
 
@@ -286,7 +295,9 @@ def tile_complexchannelattn_pa_kernel(tc, hq, hk, wq2, wk2, out):
             h_quantise(K, 0, h_grouped0, b)
 
         w_regroup(nc.vector.tensor_copy, K, 0, w_grouped0, 0, HALF_CHUNK)
+        warm_up(4)
         first_slab(0)
+        warm_up(3)
         w_regroup(nc.vector.tensor_copy, K, 0, w_grouped0, HALF_CHUNK, HALF_CHUNK + P)
         w_regroup(nc.scalar.copy, K, 0, w_grouped0, HALF_CHUNK + P, K_PASS)
         w_quantise(K, 0, w_grouped0, 0, HALF_CHUNK)

@@ -40,7 +40,7 @@ def tile_complexchannelattn_pa_kernel(tc, hq, hk, wq2, wk2, out):
 
     def unit_of(unit):
         side, u = divmod(unit, IMAGES * PASSES)
-        n, part = (u % IMAGES, u // IMAGES) if side == K else (u // PASSES, u % PASSES)
+        n, part = u // PASSES, u % PASSES
         return side, n, part
 
     operands = []
@@ -108,10 +108,11 @@ def tile_complexchannelattn_pa_kernel(tc, hq, hk, wq2, wk2, out):
                         "(p e) c -> p e c", e=2))
 
         load_h(K, 0, 0)
-        for col in range(0, K_PASS, HALF_CHUNK):
-            load_w(K, 0, col)
-        for b in range(1, SLABS):
-            load_h(K, 0, b)
+        load_w(K, 0, 0)
+        load_w(K, 0, 256)
+        load_h(K, 0, 1)
+        load_h(K, 0, 2)
+        load_h(K, 0, 3)
         for kind, side, which in operands[2:]:
             if kind == "h":
                 for b in range(0, SLABS, h_step(side, which)):
@@ -121,13 +122,13 @@ def tile_complexchannelattn_pa_kernel(tc, hq, hk, wq2, wk2, out):
                     load_w(side, which, col)
 
         make_identity(nc, ident[:])
-        heat = keep.tile([P, C], BF16, name="heat")
-        nc.vector.memset(heat[:], 0.0)
+        heat = keep.tile([P, 2 * P], BF16, name="heat")
+        nc.vector.memset(heat[:].bitcast(U32), 0)
 
         def warm_up(count):
             idle = z_banks.tile([P, PACK, P], F32, tag="z_banks", name="idle")
             for turn in range(count):
-                nc.tensor.matmul(out=idle[:].rearrange("p j c -> p (j c)"), lhsT=heat[:, :P], rhs=heat[:],
+                nc.tensor.matmul(out=idle[:, 0:2, :].rearrange("p j c -> p (j c)"), lhsT=heat[:, :P], rhs=heat[:],
                                  start=True, stop=True)
 
         nc.vector.memset(warm_in[:], 0.0)
@@ -263,8 +264,6 @@ def tile_complexchannelattn_pa_kernel(tc, hq, hk, wq2, wk2, out):
             squashed[unit] = a_stage.tile([P, PACK * C], BF16, name="squashed", align_bytes=64)
             for i in range(SLABS):
                 bank(unit, i)
-                if unit == 0 and i == 1:
-                    transposes(*prep[0])
                 if unit >= SCORE_LAG and unit_of(unit - SCORE_LAG)[0] == Q:
                     n, part = unit_of(unit - SCORE_LAG)[1:]
                     for x in range(2*i, min(2*i + 2, SLABS)) if n else (i,):
@@ -275,44 +274,52 @@ def tile_complexchannelattn_pa_kernel(tc, hq, hk, wq2, wk2, out):
                     maximum(unit - UNITS + 2)
                 if i == 0 and unit_of(unit - 1)[0] == Q and unit - 1 < 15:
                     a_quantise(unit - 1, 0, SLABS)
+                step = 2 * (unit - (UNITS - 3)) + i // 2 - 1
+                if i % 2 == 0 and 0 < step <= 4:
+                    invert(*TILES[step - 1])
+                    normalise(nc.vector, *TILES[step - 1])
                 if unit >= 15:
                     a_quantise(unit, i, i + 1)
                 if unit >= UNITS - 2 and i == 1:
                     shift(unit - UNITS + 2)
-                step = 2 * (unit - (UNITS - 3)) + i // 2 - 1
                 if i % 2 == 1 and 0 <= step < 4:
                     exponentials(*TILES[step])
-                if i % 2 == 0 and 0 < step <= 4:
-                    invert(*TILES[step - 1])
-                    normalise(nc.vector, *TILES[step - 1])
 
         h_grouped0 = h_stage.tile([P, PACK * C], BF16, name="h_grouped", align_bytes=64)
         w_grouped0 = w_stage.tile([P, K_PASS, PACK], BF16, name="w_grouped", align_bytes=64)
 
-        def first_slab(b):
-            planes = h_transposes(K, 0, b)
-            h_copy(nc.scalar.copy, K, 0, planes, h_grouped0, b)
-            h_quantise(K, 0, h_grouped0, b)
-
-        w_regroup(nc.vector.tensor_copy, K, 0, w_grouped0, 0, HALF_CHUNK)
-        warm_up(4)
-        first_slab(0)
-        warm_up(3)
-        w_regroup(nc.vector.tensor_copy, K, 0, w_grouped0, HALF_CHUNK, HALF_CHUNK + P)
-        w_regroup(nc.scalar.copy, K, 0, w_grouped0, HALF_CHUNK + P, K_PASS)
-        w_quantise(K, 0, w_grouped0, 0, HALF_CHUNK)
-        w_quantise(K, 0, w_grouped0, HALF_CHUNK, K_PASS)
-        for b in range(1, SLABS):
-            first_slab(b)
-
-        prep = operands[2:9] + [operands[11]] + operands[9:11]
+        w_grouped1 = w_stage.tile([P, K_PASS, PACK], BF16, name="w_grouped", align_bytes=64)
+        w_regroup(nc.vector.tensor_copy, K, 0, w_grouped0, 0, 256)
+        warm_up(8)
+        pl0 = h_transposes(K, 0, 0)
+        h_copy(nc.scalar.copy, K, 0, pl0, h_grouped0, 0)
+        h_quantise(K, 0, h_grouped0, 0)
+        warm_up(7)
+        w_regroup(nc.vector.tensor_copy, K, 0, w_grouped0, 256, 384)
+        w_regroup(nc.scalar.copy, K, 0, w_grouped0, 384, 512)
+        w_quantise(K, 0, w_grouped0, 0, 256)
+        w_quantise(K, 0, w_grouped0, 256, 512)
+        pl1 = h_transposes(K, 0, 1)
+        h_copy(nc.scalar.copy, K, 0, pl1, h_grouped0, 1)
+        h_quantise(K, 0, h_grouped0, 1)
+        w_regroup(nc.vector.tensor_copy, K, 1, w_grouped1, 0, 256)
+        pl2 = h_transposes(K, 0, 2)
+        h_copy(nc.scalar.copy, K, 0, pl2, h_grouped0, 2)
+        h_quantise(K, 0, h_grouped0, 2)
+        pl3 = h_transposes(K, 0, 3)
+        h_copy(nc.scalar.copy, K, 0, pl3, h_grouped0, 3)
+        h_quantise(K, 0, h_grouped0, 3)
+        w_regroup(nc.vector.tensor_copy, K, 1, w_grouped1, 256, 512)
+        w_quantise(K, 1, w_grouped1, 0, 256)
+        w_quantise(K, 1, w_grouped1, 256, 512)
+        prep = [None] + operands[3:9] + [operands[11]] + operands[9:11]
         for unit in range(UNITS):
             for n in range(IMAGES):
                 q = unit - Q_LAG[n]
                 if q >= 0 and unit_of(q)[:2] == (K, n):
                     a_quantise(q, 0, SLABS)
             run_unit(unit)
-            if unit < len(prep):
+            if unit < len(prep) and prep[unit]:
                 prepare(*prep[unit])
             if unit + 1 < len(prep):
                 transposes(*prep[unit + 1])

@@ -26,6 +26,10 @@ K = 0
 Q = 1
 UNITS = 2 * IMAGES * PASSES
 TRB = 1
+EXP_LAG = 4
+WEAVE = 14
+EB = 0
+NB = 1
 Q_LAG = (6, 6)
 SCORE_LAG = 2
 SHIFT = 24.0
@@ -60,9 +64,9 @@ def tile_complexchannelattn_pa_kernel(tc, hq, hk, wq2, wk2, out):
         keep = ctx.enter_context(tc.tile_pool(name="keep", bufs=1))
         w_stage = ctx.enter_context(tc.tile_pool(name="w_stage", bufs=2))
         h_stage = ctx.enter_context(tc.tile_pool(name="h_stage", bufs=2))
-        a_stage = ctx.enter_context(tc.tile_pool(name="a_stage", bufs=12))
-        z_banks = ctx.enter_context(tc.psum_pool(name="z_banks", bufs=4))
-        s_banks = ctx.enter_context(tc.psum_pool(name="s_banks", bufs=4))
+        a_stage = ctx.enter_context(tc.tile_pool(name="a_stage", bufs=UNITS))
+        z_banks = ctx.enter_context(tc.psum_pool(name="z_banks", bufs=5))
+        s_banks = ctx.enter_context(tc.psum_pool(name="s_banks", bufs=3))
         ctx.enter_context(tc.manual_schedule())
 
         h_raw = {(side, n, b): keep.tile([P, h_step(side, n) * R], BF16, name="h_raw%d%d%d" % (side, n, b))
@@ -80,7 +84,6 @@ def tile_complexchannelattn_pa_kernel(tc, hq, hk, wq2, wk2, out):
                     for n in range(IMAGES)] for side in (K, Q)]
         a_scales = [[keep.tile([P, PASSES, C], U8, name="a_scales%d%d" % (side, n), align_bytes=64)
                      for n in range(IMAGES)] for side in (K, Q)]
-        s_parked = [keep.tile([P, C], F32, name="s_parked%d" % m) for m in range(SLABS)]
         probs = [[keep.tile([P, C], F32, name="probs%d%d" % (n, m)) for m in range(SLABS)]
                  for n in range(IMAGES)]
 
@@ -196,33 +199,29 @@ def tile_complexchannelattn_pa_kernel(tc, hq, hk, wq2, wk2, out):
 
         def score_pass(n, g, m):
             if g == 0:
-                s_open[(n, m)] = s_banks.tile([P, C], F32, tag="s_banks", name="s")
-            part, i = (m, g) if n == 1 else (g, m)
-            words = slice(P * i, P * (i + 1))
+                if (n, m) >= (1, 2):
+                    s_open[(n, m)] = z_banks.tile([P, C], F32, tag="z_banks", name="s")
+                else:
+                    s_open[(n, m)] = s_banks.tile([P, C], F32, tag="s_banks", name="s")
+            words = slice(P * g, P * (g + 1))
             nc.tensor.matmul_mx(out=s_open[(n, m)][:],
-                                lhsT=a_codes[Q][n][:, part, words].bitcast(FP8X4),
-                                lhsT_scale=a_scales[Q][n][:, part, words],
+                                lhsT=a_codes[Q][n][:, m, words].bitcast(FP8X4),
+                                lhsT_scale=a_scales[Q][n][:, m, words],
                                 rhs=a_codes[K][n][:, g, :].bitcast(FP8X4),
                                 rhs_scale=a_scales[K][n][:, g, :],
                                 start=(g == 0), stop=(g == PASSES - 1))
 
-        def park(m):
-            nc.vector.tensor_scalar(out=s_parked[m][:], in0=s_open[(0, m)][:], scalar1=inv, scalar2=None,
-                                    op0=ALU.mult, op1=ALU.max, accum_out=row_max[0][m][:])
-            nc.vector.tensor_scalar(out=offset[0][m][:], in0=row_max[0][m][:], scalar1=-1.0, scalar2=-SHIFT,
-                                    op0=ALU.mult, op1=ALU.add)
-
-        def maximum(m):
-            nc.vector.tensor_reduce(out=row_max[1][m][:], in_=s_open[(1, m)][:],
+        def maximum(n, m):
+            nc.vector.tensor_reduce(out=row_max[n][m][:], in_=s_open[(n, m)][:],
                                     axis=mybir.AxisListType.X, op=ALU.max)
 
-        def shift(m):
-            nc.vector.tensor_scalar(out=offset[1][m][:], in0=row_max[1][m][:], scalar1=-inv, scalar2=-SHIFT,
+        def shift(n, m):
+            nc.vector.tensor_scalar(out=offset[n][m][:], in0=row_max[n][m][:], scalar1=-inv, scalar2=-SHIFT,
                                     op0=ALU.mult, op1=ALU.add)
 
         def exponentials(n, m):
-            nc.scalar.activation(out=probs[n][m][:], in_=(s_parked[m] if n == 0 else s_open[(n, m)])[:],
-                                 func=SIGMOID, bias=offset[n][m][:], scale=(1.0 if n == 0 else inv),
+            nc.scalar.activation(out=probs[n][m][:], in_=s_open[(n, m)][:],
+                                 func=SIGMOID, bias=offset[n][m][:], scale=inv,
                                  accum_out=row_sum[n][m][:])
 
         def invert(n, m):
@@ -243,7 +242,7 @@ def tile_complexchannelattn_pa_kernel(tc, hq, hk, wq2, wk2, out):
 
         def bank(unit, i):
             side, n, part = unit_of(unit)
-            g, b = (i, part) if (side, n) == (Q, 1) else (part, i)
+            g, b = (i, part) if side == Q else (part, i)
             z = z_banks.tile([P, PACK, P], F32, tag="z_banks", name="z")
             channels = slice(P * b, P * (b + 1))
             for j in range(PACK):
@@ -258,32 +257,32 @@ def tile_complexchannelattn_pa_kernel(tc, hq, hk, wq2, wk2, out):
                 out=squashed[unit][:, PACK * P * i:PACK * P * (i + 1)].rearrange("p (c j) -> p c j", j=PACK),
                 in_=z[:].rearrange("p j c -> p c j"), func=SIGMOID)
 
-        TILES = [(n, m) for n in range(IMAGES) for m in range(SLABS)]
-
         def run_unit(unit):
             squashed[unit] = a_stage.tile([P, PACK * C], BF16, name="squashed", align_bytes=64)
             for i in range(SLABS):
                 bank(unit, i)
                 if unit >= SCORE_LAG and unit_of(unit - SCORE_LAG)[0] == Q:
-                    n, part = unit_of(unit - SCORE_LAG)[1:]
-                    for x in range(2*i, min(2*i + 2, SLABS)) if n else (i,):
-                        score_pass(n, x if n else part, part if n else x)
-                        if (n, part) == (0, PASSES - 1):
-                            park(x)
-                if unit >= UNITS - 2 and i == 1:
-                    maximum(unit - UNITS + 2)
-                if i == 0 and unit_of(unit - 1)[0] == Q and unit - 1 < 15:
+                    tile = unit_of(unit - SCORE_LAG)[1:]
+                    W = 2 if unit >= WEAVE else 1
+                    for g in range(W*i, min(W*i + W, SLABS)):
+                        score_pass(tile[0], g, tile[1])
+                    if i == SLABS // W - 1:
+                        maximum(*tile)
+                if i == 0 and unit_of(unit - 1)[0] == Q and unit - 1 < UNITS - 1:
                     a_quantise(unit - 1, 0, SLABS)
-                step = 2 * (unit - (UNITS - 3)) + i // 2 - 1
-                if i % 2 == 0 and 0 < step <= 4:
-                    invert(*TILES[step - 1])
-                    normalise(nc.vector, *TILES[step - 1])
-                if unit >= 15:
+                if i == NB and unit >= 2 * PASSES + EXP_LAG:
+                    invert(*unit_of(unit - EXP_LAG)[1:])
+                    normalise(nc.vector, *unit_of(unit - EXP_LAG)[1:])
+                if unit == UNITS - 1:
+                    if i == SLABS - 1:
+                        for g in range(PASSES):
+                            score_pass(1, g, 2)
+                        maximum(1, 2)
                     a_quantise(unit, i, i + 1)
-                if unit >= UNITS - 2 and i == 1:
-                    shift(unit - UNITS + 2)
-                if i % 2 == 1 and 0 <= step < 4:
-                    exponentials(*TILES[step])
+                if unit >= SCORE_LAG and unit_of(unit - SCORE_LAG)[0] == Q and i == SLABS // W - 1:
+                    shift(*tile)
+                if i == EB and unit >= 2 * PASSES + EXP_LAG:
+                    exponentials(*unit_of(unit - EXP_LAG)[1:])
 
         h_grouped0 = h_stage.tile([P, PACK * C], BF16, name="h_grouped", align_bytes=64)
         w_grouped0 = w_stage.tile([P, K_PASS, PACK], BF16, name="w_grouped", align_bytes=64)
@@ -312,32 +311,29 @@ def tile_complexchannelattn_pa_kernel(tc, hq, hk, wq2, wk2, out):
         w_regroup(nc.vector.tensor_copy, K, 1, w_grouped1, 256, 512)
         w_quantise(K, 1, w_grouped1, 0, 256)
         w_quantise(K, 1, w_grouped1, 256, 512)
-        prep = [None] + operands[3:9] + [operands[11]] + operands[9:11]
+        PR = {1: (3,), 2: (4,), 3: (5,), 4: (6,), 5: (7,), 6: (8,), 7: (9, 10, 11)}
+        TRS = {2: (5,), 3: (6,), 6: (11,)}
+        KQ = {8: (0, 1, 2, 3), 10: (4, 5), 11: (6, 7)}
         for unit in range(UNITS):
-            for n in range(IMAGES):
-                q = unit - Q_LAG[n]
-                if q >= 0 and unit_of(q)[:2] == (K, n):
-                    a_quantise(q, 0, SLABS)
+            for k in KQ.get(unit, ()):
+                a_quantise(k, 0, SLABS)
             run_unit(unit)
-            if unit < len(prep) and prep[unit]:
-                prepare(*prep[unit])
-            if unit + 1 < len(prep):
-                transposes(*prep[unit + 1])
+            for op in PR.get(unit, ()):
+                prepare(*operands[op])
+            for op in TRS.get(unit, ()):
+                transposes(*operands[op])
 
         exponentials(1, 0)
         exponentials(1, 1)
-        for g in range(PASSES):
-            score_pass(1, g, 2)
-        maximum(2)
-        invert(1, 0)
-        shift(2)
+        shift(1, 2)
         exponentials(1, 2)
+        invert(1, 0)
         normalise(nc.vector, 1, 0)
         for g in range(PASSES):
             score_pass(1, g, 3)
-        maximum(3)
+        maximum(1, 3)
         invert(1, 1)
-        shift(3)
+        shift(1, 3)
         exponentials(1, 3)
         normalise(nc.vector, 1, 1)
         invert(1, 2)

@@ -293,7 +293,7 @@ def tile_complexchannelattn_pa_kernel(tc, hq, hk, wq2, wk2, out):
         pl0 = h_transposes(K, 0, 0)
         h_copy(nc.scalar.copy, K, 0, pl0, h_grouped0, 0)
         h_quantise(K, 0, h_grouped0, 0)
-        warm_up(7)
+        warm_up(4)
         w_regroup(nc.vector.tensor_copy, K, 0, w_grouped0, 256, 384)
         w_regroup(nc.scalar.copy, K, 0, w_grouped0, 384, 512)
         w_quantise(K, 0, w_grouped0, 0, 256)

@@ -263,10 +263,11 @@ def tile_complexchannelattn_pa_kernel(tc, hq, hk, wq2, wk2, out):
                 bank(unit, i)
                 if unit >= SCORE_LAG and unit_of(unit - SCORE_LAG)[0] == Q:
                     tile = unit_of(unit - SCORE_LAG)[1:]
-                    W = 2 if unit >= WEAVE else 1
-                    for g in range(W*i, min(W*i + W, SLABS)):
-                        score_pass(tile[0], g, tile[1])
-                    if i == SLABS // W - 1:
+                    o = 0 if unit >= WEAVE else 2
+                    for g in range(2 * (i - o), 2 * (i - o) + 2):
+                        if 0 <= g < PASSES:
+                            score_pass(tile[0], g, tile[1])
+                    if i == o + 1:
                         maximum(*tile)
                 if i == 0 and unit_of(unit - 1)[0] == Q and unit - 1 < UNITS - 1:
                     a_quantise(unit - 1, 0, SLABS)
@@ -279,7 +280,7 @@ def tile_complexchannelattn_pa_kernel(tc, hq, hk, wq2, wk2, out):
                             score_pass(1, g, 2)
                         maximum(1, 2)
                     a_quantise(unit, i, i + 1)
-                if unit >= SCORE_LAG and unit_of(unit - SCORE_LAG)[0] == Q and i == SLABS // W - 1:
+                if unit >= SCORE_LAG and unit_of(unit - SCORE_LAG)[0] == Q and i == o + 1:
                     shift(*tile)
                 if i == EB and unit >= 2 * PASSES + EXP_LAG:
                     exponentials(*unit_of(unit - EXP_LAG)[1:])

from contextlib import ExitStack
import math

import concourse.mybir as mybir
from concourse.masks import make_identity

F32 = mybir.dt.float32
BF16 = mybir.dt.bfloat16
U32 = mybir.dt.uint32
U8 = mybir.dt.uint8
FP8X4 = mybir.dt.float8_e4m3fn_x4
SIGMOID = mybir.ActivationFunctionType.Sigmoid
ALU = mybir.AluOpType

P = 128
PACK = 4
K_PASS = P * PACK
IMAGES = 2
C = 512
R = 512
HW = 2048
PASSES = HW // K_PASS
HALF_CHUNK = K_PASS // 2
SLABS = C // P
K = 0
Q = 1
UNITS = 2 * IMAGES * PASSES
TRB = 1
EXP_LAG = 4
WEAVE = 14
EB = 0
NB = 1
Q_LAG = (6, 6)
SCORE_LAG = 2
SHIFT = 24.0
FLOPS = 2 * 2 * IMAGES * C * R * HW + 2 * IMAGES * C * C * HW


def tile_complexchannelattn_pa_kernel(tc, hq, hk, wq2, wk2, out):
    nc = tc.nc
    h_dram = (hk, hq)
    w_dram = (wk2, wq2)
    inv = 1.0 / math.sqrt(C)

    def unit_of(unit):
        side, u = divmod(unit, IMAGES * PASSES)
        n, part = u // PASSES, u % PASSES
        return side, n, part

    operands = []
    for unit in range(UNITS):
        side, n, g = unit_of(unit)
        for operand in (("h", side, n), ("w", side, g)):
            if operand not in operands:
                operands.append(operand)

    def h_step(side, n):
        return 1 if side == K else 2

    def w_step(side, g):
        return HALF_CHUNK if side == K and g < 2 else K_PASS

    with ExitStack() as ctx:
        keep = ctx.enter_context(tc.tile_pool(name="keep", bufs=1))
        w_stage = ctx.enter_context(tc.tile_pool(name="w_stage", bufs=2))
        h_stage = ctx.enter_context(tc.tile_pool(name="h_stage", bufs=2))
        a_stage = ctx.enter_context(tc.tile_pool(name="a_stage", bufs=UNITS))
        z_banks = ctx.enter_context(tc.psum_pool(name="z_banks", bufs=5))
        s_banks = ctx.enter_context(tc.psum_pool(name="s_banks", bufs=3))
        ctx.enter_context(tc.manual_schedule())

        h_raw = {(side, n, b): keep.tile([P, h_step(side, n) * R], BF16, name="h_raw%d%d%d" % (side, n, b))
                 for side in (K, Q) for n in range(IMAGES) for b in range(0, SLABS, h_step(side, n))}
        w_raw = {(side, g, col): keep.tile([P, PACK, w_step(side, g)], BF16,
                                           name="w_raw%d%d%d" % (side, g, col))
                 for side in (K, Q) for g in range(PASSES) for col in range(0, K_PASS, w_step(side, g))}
        h_codes = [[keep.tile([P, C], U32, name="h_codes%d%d" % (side, n), align_bytes=64)
                    for n in range(IMAGES)] for side in (K, Q)]
        h_scales = [[keep.tile([P, C], U8, name="h_scales%d%d" % (side, n), align_bytes=64)
                     for n in range(IMAGES)] for side in (K, Q)]
        w_codes = [keep.tile([P, HW], U32, name="w_codes%d" % side, align_bytes=64) for side in (K, Q)]
        w_scales = [keep.tile([P, HW], U8, name="w_scales%d" % side, align_bytes=64) for side in (K, Q)]
        a_codes = [[keep.tile([P, PASSES, C], U32, name="a_codes%d%d" % (side, n), align_bytes=64)
                    for n in range(IMAGES)] for side in (K, Q)]
        a_scales = [[keep.tile([P, PASSES, C], U8, name="a_scales%d%d" % (side, n), align_bytes=64)
                     for n in range(IMAGES)] for side in (K, Q)]
        probs = [[keep.tile([P, C], F32, name="probs%d%d" % (n, m)) for m in range(SLABS)]
                 for n in range(IMAGES)]

        def per_row(name):
            return [[keep.tile([P, 1], F32, name="%s%d%d" % (name, n, m)) for m in range(SLABS)]
                    for n in range(IMAGES)]

        row_max, offset, row_sum, inv_sum = per_row("row_max"), per_row("offset"), per_row("row_sum"), per_row("inv_sum")
        ident = keep.tile([P, P], F32, name="ident")
        warm_in = keep.tile([P, 1], F32, name="warm_in")
        warm_out = keep.tile([P, 1], F32, name="warm_out")

        def load_h(side, n, b):
            slabs = h_step(side, n)
            nc.sync.dma_start(
                out=h_raw[(side, n, b)][:].rearrange("p (b r) -> p b r", b=slabs),
                in_=h_dram[side][n, P * b:P * (b + slabs), :].rearrange("(b p) r -> p b r", p=P))

        def load_w(side, g, col):
            lo = K_PASS * g + col
            for a in range(2):
                nc.sync.dma_start(
                    out=w_raw[(side, g, col)][:, 2 * a:2 * a + 2, :],
                    in_=w_dram[side][2 * P * a:2 * P * (a + 1), lo:lo + w_step(side, g)].rearrange(
                        "(p e) c -> p e c", e=2))

        load_h(K, 0, 0)
        load_w(K, 0, 0)
        load_w(K, 0, 256)
        load_h(K, 0, 1)
        load_h(K, 0, 2)
        load_h(K, 0, 3)
        for kind, side, which in operands[2:]:
            if kind == "h":
                for b in range(0, SLABS, h_step(side, which)):
                    load_h(side, which, b)
            else:
                for col in range(0, K_PASS, w_step(side, which)):
                    load_w(side, which, col)

        make_identity(nc, ident[:])
        heat = keep.tile([P, 2 * P], BF16, name="heat")
        nc.vector.memset(heat[:].bitcast(U32), 0)

        def warm_up(count):
            idle = z_banks.tile([P, PACK, P], F32, tag="z_banks", name="idle")
            for turn in range(count):
                nc.tensor.matmul(out=idle[:, 0:2, :].rearrange("p j c -> p (j c)"), lhsT=heat[:, :P], rhs=heat[:],
                                 start=True, stop=True)

        nc.vector.memset(warm_in[:], 0.0)
        nc.scalar.activation(out=warm_out[:], in_=warm_in[:], func=SIGMOID)

        def h_transposes(side, n, b0):
            slabs = h_step(side, n)
            planes = s_banks.tile([P, slabs, 2, P], F32, tag="s_banks", name="planes")
            words = h_raw[(side, n, b0)][:].bitcast(F32)
            for b in range(slabs):
                for a in range(2):
                    lo = 2 * P * b + P * a
                    nc.tensor.transpose(planes[:, b, a, :], words[:, lo:lo + P], ident[:])
            return planes

        def h_copy(copy, side, n, planes, grouped, b0):
            slabs = h_step(side, n)
            dst = grouped[:].bitcast(F32)[:, 2 * P * b0:2 * P * (b0 + slabs)]
            copy(out=dst.rearrange("p (b c a) -> p b c a", b=slabs, a=2),
                 in_=planes[:].rearrange("p b a c -> p b c a"))

        def h_quantise(side, n, grouped, b0):
            c0, c1 = P * b0, P * (b0 + h_step(side, n))
            nc.vector.quantize_mx(out=h_codes[side][n][:, c0:c1].bitcast(FP8X4),
                                  scales=h_scales[side][n][:, c0:c1],
                                  in_=grouped[:, PACK * c0:PACK * c1])

        def w_regroup(copy, side, g, grouped, col0, col1):
            base = col0 - col0 % w_step(side, g)
            copy(out=grouped[:, col0:col1, :].rearrange("p (c i) t -> p c t i", i=4),
                 in_=w_raw[(side, g, base)][:, :, col0 - base:col1 - base].rearrange(
                     "p t (c i) -> p c t i", i=4))

        def w_quantise(side, g, grouped, col0, col1):
            lo = K_PASS * g
            nc.vector.quantize_mx(out=w_codes[side][:, lo + col0:lo + col1].bitcast(FP8X4),
                                  scales=w_scales[side][:, lo + col0:lo + col1],
                                  in_=grouped[:, col0:col1, :].rearrange("p c t -> p (c t)"))

        early = {}

        def transposes(kind, side, which):
            if kind == "h":
                early[(side, which)] = [h_transposes(side, which, b) for b in range(0, SLABS, h_step(side, which))]

        def prepare(kind, side, which):
            if kind == "h":
                starts = range(0, SLABS, h_step(side, which))
                planes = early.pop((side, which))
                grouped = h_stage.tile([P, PACK * C], BF16, name="h_grouped", align_bytes=64)
                step = h_step(side, which)
                for b in starts:
                    h_copy(nc.vector.tensor_copy, side, which, planes[b // step], grouped, b)
                    if b > 0:
                        h_quantise(side, which, grouped, b - step)
                h_quantise(side, which, grouped, SLABS - step)
            else:
                grouped = w_stage.tile([P, K_PASS, PACK], BF16, name="w_grouped", align_bytes=64)
                for col in (0, HALF_CHUNK):
                    w_regroup(nc.vector.tensor_copy, side, which, grouped, col, col + HALF_CHUNK)
                for col in (0, HALF_CHUNK):
                    w_quantise(side, which, grouped, col, col + HALF_CHUNK)

        s_open = {}

        def score_pass(n, g, m):
            if g == 0:
                if (n, m) >= (1, 2):
                    s_open[(n, m)] = z_banks.tile([P, C], F32, tag="z_banks", name="s")
                else:
                    s_open[(n, m)] = s_banks.tile([P, C], F32, tag="s_banks", name="s")
            words = slice(P * g, P * (g + 1))
            nc.tensor.matmul_mx(out=s_open[(n, m)][:],
                                lhsT=a_codes[Q][n][:, m, words].bitcast(FP8X4),
                                lhsT_scale=a_scales[Q][n][:, m, words],
                                rhs=a_codes[K][n][:, g, :].bitcast(FP8X4),
                                rhs_scale=a_scales[K][n][:, g, :],
                                start=(g == 0), stop=(g == PASSES - 1))

        def maximum(n, m):
            nc.vector.tensor_reduce(out=row_max[n][m][:], in_=s_open[(n, m)][:],
                                    axis=mybir.AxisListType.X, op=ALU.max)

        def shift(n, m):
            nc.vector.tensor_scalar(out=offset[n][m][:], in0=row_max[n][m][:], scalar1=-inv, scalar2=-SHIFT,
                                    op0=ALU.mult, op1=ALU.add)

        def exponentials(n, m):
            nc.scalar.activation(out=probs[n][m][:], in_=s_open[(n, m)][:],
                                 func=SIGMOID, bias=offset[n][m][:], scale=inv,
                                 accum_out=row_sum[n][m][:])

        def invert(n, m):
            nc.vector.reciprocal(out=inv_sum[n][m][:], in_=row_sum[n][m][:])

        def normalise(engine, n, m):
            engine.tensor_scalar(out=probs[n][m][:], in0=probs[n][m][:], scalar1=inv_sum[n][m][:],
                                 scalar2=0.0, op0=ALU.mult, op1=ALU.add)
            nc.sync.dma_start(out=out[n, P * m:P * (m + 1), :], in_=probs[n][m][:])

        squashed = {}

        def a_quantise(unit, i0, i1):
            side, n, part = unit_of(unit)
            nc.vector.quantize_mx(out=a_codes[side][n][:, part, P * i0:P * i1].bitcast(FP8X4),
                                  scales=a_scales[side][n][:, part, P * i0:P * i1],
                                  in_=squashed[unit][:, PACK * P * i0:PACK * P * i1])

        def bank(unit, i):
            side, n, part = unit_of(unit)
            g, b = (i, part) if side == Q else (part, i)
            z = z_banks.tile([P, PACK, P], F32, tag="z_banks", name="z")
            channels = slice(P * b, P * (b + 1))
            for j in range(PACK):
                positions = slice(K_PASS * g + P * j, K_PASS * g + P * (j + 1))
                nc.tensor.matmul_mx(out=z[:, j, :],
                                    lhsT=w_codes[side][:, positions].bitcast(FP8X4),
                                    lhsT_scale=w_scales[side][:, positions],
                                    rhs=h_codes[side][n][:, channels].bitcast(FP8X4),
                                    rhs_scale=h_scales[side][n][:, channels],
                                    start=True, stop=True)
            nc.scalar.activation(
                out=squashed[unit][:, PACK * P * i:PACK * P * (i + 1)].rearrange("p (c j) -> p c j", j=PACK),
                in_=z[:].rearrange("p j c -> p c j"), func=SIGMOID)

        def run_unit(unit):
            squashed[unit] = a_stage.tile([P, PACK * C], BF16, name="squashed", align_bytes=64)
            for i in range(SLABS):
                bank(unit, i)
                if unit >= SCORE_LAG and unit_of(unit - SCORE_LAG)[0] == Q:
                    tile = unit_of(unit - SCORE_LAG)[1:]
                    o = 0 if unit >= WEAVE else 2
                    for g in range(2 * (i - o), 2 * (i - o) + 2):
                        if 0 <= g < PASSES:
                            score_pass(tile[0], g, tile[1])
                    if i == o + 1:
                        maximum(*tile)
                if i == 0 and unit_of(unit - 1)[0] == Q and unit - 1 < UNITS - 1:
                    a_quantise(unit - 1, 0, SLABS)
                if i == NB and unit >= 2 * PASSES + EXP_LAG:
                    invert(*unit_of(unit - EXP_LAG)[1:])
                    normalise(nc.vector, *unit_of(unit - EXP_LAG)[1:])
                if unit == UNITS - 1:
                    if i == SLABS - 1:
                        for g in range(PASSES):
                            score_pass(1, g, 2)
                        maximum(1, 2)
                    a_quantise(unit, i, i + 1)
                if unit >= SCORE_LAG and unit_of(unit - SCORE_LAG)[0] == Q and i == o + 1:
                    shift(*tile)
                if i == EB and unit >= 2 * PASSES + EXP_LAG:
                    exponentials(*unit_of(unit - EXP_LAG)[1:])

        h_grouped0 = h_stage.tile([P, PACK * C], BF16, name="h_grouped", align_bytes=64)
        w_grouped0 = w_stage.tile([P, K_PASS, PACK], BF16, name="w_grouped", align_bytes=64)

        w_grouped1 = w_stage.tile([P, K_PASS, PACK], BF16, name="w_grouped", align_bytes=64)
        w_regroup(nc.vector.tensor_copy, K, 0, w_grouped0, 0, 256)
        warm_up(8)
        pl0 = h_transposes(K, 0, 0)
        h_copy(nc.scalar.copy, K, 0, pl0, h_grouped0, 0)
        h_quantise(K, 0, h_grouped0, 0)
        warm_up(4)
        w_regroup(nc.vector.tensor_copy, K, 0, w_grouped0, 256, 384)
        w_regroup(nc.scalar.copy, K, 0, w_grouped0, 384, 512)
        w_quantise(K, 0, w_grouped0, 0, 256)
        w_quantise(K, 0, w_grouped0, 256, 512)
        pl1 = h_transposes(K, 0, 1)
        h_copy(nc.scalar.copy, K, 0, pl1, h_grouped0, 1)
        h_quantise(K, 0, h_grouped0, 1)
        w_regroup(nc.vector.tensor_copy, K, 1, w_grouped1, 0, 256)
        pl2 = h_transposes(K, 0, 2)
        h_copy(nc.scalar.copy, K, 0, pl2, h_grouped0, 2)
        h_quantise(K, 0, h_grouped0, 2)
        pl3 = h_transposes(K, 0, 3)
        h_copy(nc.scalar.copy, K, 0, pl3, h_grouped0, 3)
        h_quantise(K, 0, h_grouped0, 3)
        w_regroup(nc.vector.tensor_copy, K, 1, w_grouped1, 256, 512)
        w_quantise(K, 1, w_grouped1, 0, 256)
        w_quantise(K, 1, w_grouped1, 256, 512)
        PR = {1: (3,), 2: (4,), 3: (5,), 4: (6,), 5: (7,), 6: (8,), 7: (9, 10, 11)}
        TRS = {2: (5,), 3: (6,), 6: (11,)}
        KQ = {8: (0, 1, 2, 3), 10: (4, 5), 11: (6, 7)}
        for unit in range(UNITS):
            for k in KQ.get(unit, ()):
                a_quantise(k, 0, SLABS)
            run_unit(unit)
            for op in PR.get(unit, ()):
                prepare(*operands[op])
            for op in TRS.get(unit, ()):
                transposes(*operands[op])

        exponentials(1, 0)
        exponentials(1, 1)
        shift(1, 2)
        exponentials(1, 2)
        invert(1, 0)
        normalise(nc.vector, 1, 0)
        for g in range(PASSES):
            score_pass(1, g, 3)
        maximum(1, 3)
        invert(1, 1)
        shift(1, 3)
        exponentials(1, 3)
        normalise(nc.vector, 1, 1)
        invert(1, 2)
        normalise(nc.vector, 1, 2)
        invert(1, 3)
        normalise(nc.vector, 1, 3)
